import numpy as np
import ml_dtypes


def mxq(x, axis, fmt="e4m3"):
    dtype, down = {"e4m3": (ml_dtypes.float8_e4m3fn, 7), "e5m2": (ml_dtypes.float8_e5m2, 14)}[fmt]
    v = np.moveaxis(np.asarray(x, np.float32).astype(ml_dtypes.bfloat16).astype(np.float64), axis, -1)
    blocks = v.reshape(v.shape[:-1] + (-1, 32))
    amax = np.abs(blocks).max(-1, keepdims=True)
    byte = np.maximum(np.where(amax > 0, np.frexp(amax)[1] - 1 + 127, 0) - down, 1)
    scale = np.exp2(byte - 127.0)
    codes = (blocks / scale).astype(np.float32).astype(dtype).astype(np.float64)
    return np.moveaxis((codes * scale).reshape(v.shape), -1, axis)


WIDE = False


def mx_kscale(k):
    if not WIDE:
        return np.ones(k)
    levels = np.array([10, -10, 5, -5, 0])
    if k % 512:
        return np.exp2(np.random.permutation(np.resize(levels, k // 32))).repeat(32)
    a = np.empty((k // 512, 16))
    for p in range(k // 512):
        a[p, :8] = np.random.permutation(np.resize(levels, 8))
        for g in range(8):
            far = levels[np.abs(levels - a[p, g]) >= 10]
            a[p, g + 8] = far[np.random.randint(len(far))]
    return np.exp2(a.ravel()).repeat(32)


BF16 = ml_dtypes.bfloat16


def bf(x):
    return np.asarray(x, np.float32).astype(BF16)


def f64(x):
    return np.asarray(x).astype(np.float64)


B, F0, FK, S1, S2, D = 64, 64, 128, 128, 128, 16
M1 = F0 * FK
M2 = F0 * S1


def setup_inputs():
    u = mx_kscale(M2).reshape(F0, S1)[:, 0]
    t = mx_kscale(M1).reshape(F0, FK)[0]
    w1 = np.random.standard_normal((F0, FK, S1)) / np.sqrt(M1) / u[:, None, None] / t[None, :, None]
    w2 = np.random.standard_normal((F0, S1, S2)) / np.sqrt(M2) / u[:, None, None]
    return {"x": bf(np.random.standard_normal((B, F0, D)) * u[None, :, None]),
            "x1": bf(np.random.standard_normal((B, FK, D)) * t[None, :, None]),
            "w1": bf(w1.reshape(M1, S1)), "b1": bf(np.random.standard_normal(S1) * 0.2),
            "w2": bf(w2.reshape(M2, S2)), "b2": bf(np.random.standard_normal(S2) * 0.2)}


def reference(x, x1, w1, b1, w2, b2):
    x0 = f64(x).transpose(0, 2, 1)
    xk = f64(x1).transpose(0, 2, 1)
    z1 = (x0[:, :, :, None] * xk[:, :, None, :]).reshape(B, D, M1)
    o1 = (mxq(z1, 2, "e4m3") @ mxq(f64(w1), 0, "e4m3")) + f64(b1)
    z2 = (x0[:, :, :, None] * o1[:, :, None, :]).reshape(B, D, M2)
    o2 = (mxq(z2, 2, "e4m3") @ mxq(f64(w2), 0, "e4m3")) + f64(b2)
    return np.concatenate([o1.sum(axis=1), o2.sum(axis=1)], axis=1)

@@ -1,0 +1,289 @@
+from contextlib import ExitStack
+
+import concourse.mybir as mybir
+from concourse.masks import make_identity
+
+F32 = mybir.dt.float32
+BF16 = mybir.dt.bfloat16
+U32 = mybir.dt.uint32
+U8 = mybir.dt.uint8
+FP8X4 = mybir.dt.float8_e4m3fn_x4
+MULT = mybir.AluOpType.mult
+ADD = mybir.AluOpType.add
+COPY = mybir.ActivationFunctionType.Copy
+
+P = 128
+B, F0, FK, S, D = 64, 64, 128, 128, 16
+N = B * D
+K = F0 * FK
+K_PASS = 4 * P
+PASSES = K // K_PASS
+N_TILES = N // P
+B_TILE = P // D
+CHUNK = 4
+CHUNKS = PASSES // CHUNK
+I_PASS = K_PASS // FK
+I_CHUNK = CHUNK * I_PASS
+LAYERS = 2
+QUADS = 4
+QUAD = P // QUADS
+LEAD = 6
+SCALAR_EVERY_BESIDE = 2
+SCALAR_EVERY_ALONE = 4
+
+FLOPS = LAYERS * 2 * N * K * S
+
+
+def tile_cin_pa_kernel(tc, x, x1, w1, b1, w2, b2, out):
+    nc = tc.nc
+    with ExitStack() as stack:
+        keep = stack.enter_context(tc.tile_pool(name="keep", bufs=1))
+        stage = stack.enter_context(tc.tile_pool(name="stage", bufs=3))
+
+        x_fields = keep.tile([P, N // 2], BF16)
+        for h in range(2):
+            nc.sync.dma_start(
+                out=x_fields[F0 * h : F0 * (h + 1), :].rearrange("i (b d) -> i b d", d=D),
+                in_=x[B // 2 * h : B // 2 * (h + 1)].rearrange("b i d -> i b d"),
+            )
+        x1_fields = keep.tile([P, N], BF16)
+
+        def load_x1(quarter):
+            nc.sync.dma_start(
+                out=x1_fields[:, N // 4 * quarter : N // 4 * (quarter + 1)].rearrange("j (b d) -> j b d", d=D),
+                in_=x1[B // 4 * quarter : B // 4 * (quarter + 1)].rearrange("b j d -> j b d"),
+            )
+
+        w_rows = [keep.tile([P, PASSES, 4, S], BF16, name="w_rows%d" % l) for l in range(LAYERS)]
+
+        def load_weights(layer):
+            source = (w1, w2)[layer].rearrange("(c g p t) s -> p c g (t s)", c=CHUNKS, p=P, t=4)
+            for c in range(CHUNKS):
+                rows = w_rows[layer][:, CHUNK * c : CHUNK * (c + 1), :, :]
+                nc.sync.dma_start(out=rows.rearrange("p g t s -> p g (t s)"), in_=source[:, c, :, :])
+
+        load_x1(0)
+        bias_bf = keep.tile([P, LAYERS, S], BF16)
+        nc.sync.dma_start(out=bias_bf[:, 0, :], in_=b1.partition_broadcast(P))
+        nc.sync.dma_start(out=bias_bf[:, 1, :], in_=b2.partition_broadcast(P))
+        load_weights(0)
+        load_x1(1)
+        load_weights(1)
+        load_x1(2)
+        load_x1(3)
+
+        ident_bf = keep.tile([P, P], BF16)
+        make_identity(nc, ident_bf[:])
+        ident_f = keep.tile([P, P], F32)
+        make_identity(nc, ident_f[:])
+        pool_first = B - B_TILE
+        pool_sel = keep.tile([P, pool_first + P], F32)
+        nc.vector.memset(pool_sel[:], 0.0)
+        nc.vector.tensor_reduce(
+            out=pool_sel[:, pool_first : pool_first + B_TILE],
+            in_=ident_f[:].rearrange("p (b d) -> p b d", d=D),
+            axis=mybir.AxisListType.X,
+            op=ADD,
+        )
+        b1_rows = keep.tile([P, S], F32)
+        nc.vector.tensor_copy(
+            out=b1_rows[:].rearrange("p (u r e) -> p u r e", u=2, e=2),
+            in_=bias_bf[:, 0, :].rearrange("p (r u e) -> p u r e", u=2, e=2),
+        )
+        late_bias = keep.tile([P, S], F32)
+        nc.vector.tensor_scalar(out=late_bias[:], in0=bias_bf[:, 1, :], scalar1=float(D), scalar2=None, op0=MULT)
+
+        x_scalar = keep.tile([P, 4, 2, F0], F32)
+        x_pairs = keep.tile([P, 4, 2, F0, 2], BF16)
+        x1_spread = keep.tile([P, N_TILES * P * 4], BF16)
+        x1_spread_words = x1_spread[:].bitcast(F32).rearrange("p (a n h) -> p a n h", a=N_TILES, h=2)
+        turn = stack.enter_context(tc.psum_pool(name="turn", bufs=4))
+        x_t = turn.tile([P, 4, P], BF16, tag="bank")
+        for m in range(4):
+            nc.tensor.transpose(x_t[:, m, :], x_fields[:, P * m : P * (m + 1)], ident_bf[:])
+        x_flat = x_t[:].rearrange("p m c -> p (m c)")
+        nc.vector.tensor_copy(out=x_scalar[:].rearrange("p m h i -> p (m h i)"), in_=x_flat)
+        nc.scalar.copy(
+            out=x_pairs[:].rearrange("p m h i r -> p (m h i) r"),
+            in_=x_flat.unsqueeze(2).to_broadcast([P, 4 * P, 2]),
+        )
+
+        def turn_x1(quarter):
+            x1_t = turn.tile([P, 2, P], BF16, tag="bank")
+            x1_copies = stage.tile([P, 2, 2, QUADS, QUAD], F32)
+            for a in range(2):
+                t = 2 * quarter + a
+                nc.tensor.transpose(x1_t[:, a, :], x1_fields[:, P * t : P * (t + 1)], ident_bf[:])
+            for a in range(2):
+                nc.scalar.copy(
+                    out=x1_copies[:, a, :, :, :],
+                    in_=x1_t[:, a, :].bitcast(F32).rearrange("p (r h) -> p h r", h=2).unsqueeze(2)
+                    .to_broadcast([P, 2, QUADS, QUAD]),
+                )
+            bank = turn.tile([P, 2, 2, P], F32, tag="bank")
+            for a in range(2):
+                for h in range(2):
+                    nc.tensor.transpose(
+                        bank[:, a, h, :], x1_copies[:, a, h, :, :].rearrange("p q r -> p (q r)"), ident_f[:]
+                    )
+            nc.scalar.copy(
+                out=x1_spread_words[:, 2 * quarter : 2 * quarter + 2, :, :],
+                in_=bank[:].rearrange("p a h n -> p a n h"),
+            )
+
+        turn_x1(0)
+
+        sums = stack.enter_context(tc.psum_pool(name="sums", bufs=3))
+        total = stack.enter_context(tc.psum_pool(name="total", bufs=1))
+
+        w_codes = [keep.tile([P, PASSES, S], U32, name="w_codes%d" % l, align_bytes=64) for l in range(LAYERS)]
+        w_scales = [keep.tile([P, PASSES, S], U8, name="w_scales%d" % l, align_bytes=64) for l in range(LAYERS)]
+        pooled = total.tile([P, LAYERS * S], F32)
+
+        def prepare_weights(layer, first, count, copy):
+            w_grouped = stage.tile([P, count, S, 4], BF16, align_bytes=64, tag="w_grouped%d" % count)
+            copy(
+                out=w_grouped[:],
+                in_=w_rows[layer][:, first : first + count, :, :].rearrange("p g t s -> p g s t"),
+            )
+            nc.vector.quantize_mx(
+                out=w_codes[layer][:, first : first + count, :].rearrange("p g s -> p (g s)").bitcast(FP8X4),
+                scales=w_scales[layer][:, first : first + count, :].rearrange("p g s -> p (g s)"),
+                in_=w_grouped[:].rearrange("p g s t -> p (g s t)"),
+            )
+
+        per_layer = [[(layer, t, c) for t in range(N_TILES) for c in range(CHUNKS)] for layer in range(LAYERS)]
+        chunks = []
+        for k in range(N_TILES * CHUNKS + LEAD):
+            if k < N_TILES * CHUNKS:
+                chunks.append(per_layer[0][k])
+            if k >= LEAD:
+                chunks.append(per_layer[1][k - LEAD])
+        last_of_layer_1 = chunks.index(per_layer[0][-1])
+
+        rows_n, z_grouped, z_codes, z_scales, acc, o12 = {}, {}, {}, {}, {}, {}
+
+        def start_chunk(step):
+            layer, t, c = chunks[step]
+            m, h = t % 4, t // 4
+            first_i = I_CHUNK * c
+            if layer == 0:
+                x_copies = stage.tile([P, CHUNK, QUADS, QUAD], F32)
+                rows_n[step] = x_copies
+                words = x_pairs[:, m, h, first_i : first_i + I_CHUNK, :].rearrange("p i r -> p (i r)").bitcast(F32)
+                nc.scalar.copy(
+                    out=x_copies[:],
+                    in_=words.rearrange("p (a q) -> p a q", q=QUADS).unsqueeze(3).to_broadcast([P, CHUNK, QUADS, QUAD]),
+                )
+                return
+            z = stage.tile([P, I_CHUNK * FK], BF16, name="z_rows")
+            rows_n[step] = z
+            every = SCALAR_EVERY_BESIDE if step < last_of_layer_1 else SCALAR_EVERY_ALONE
+            for i in range(I_CHUNK):
+                x_i = x_scalar[:, m, h, first_i + i : first_i + i + 1]
+                a, q = divmod(i, I_PASS)
+                z_i = z[:, K_PASS * a : K_PASS * (a + 1)].rearrange("p (u q w) -> p u q w", u=2, q=I_PASS)[:, :, q, :]
+                o1_t = o12[t][:, 0:S].rearrange("p (u w) -> p u w", u=2)
+                if i % every == every - 1:
+                    nc.scalar.activation(out=z_i, in_=o1_t, func=COPY, scale=x_i)
+                else:
+                    nc.vector.tensor_scalar(out=z_i, in0=o1_t, scalar1=x_i, scalar2=None, op0=MULT)
+
+        def turn_to_k(step):
+            layer, t, c = chunks[step]
+            grouped = stage.tile([P, CHUNK * P * 4], BF16, name="z_grouped", align_bytes=64)
+            z_grouped[step] = grouped
+            if layer == 0:
+                bank = turn.tile([P, CHUNK, P], F32, tag="bank")
+                for a in range(CHUNK):
+                    nc.tensor.transpose(bank[:, a, :], rows_n[step][:, a, :, :].rearrange("p q r -> p (q r)"), ident_f[:])
+                shape = [P, CHUNK, P, 2, 2]
+                nc.vector.tensor_tensor(
+                    out=grouped[:].rearrange("p (a n h l) -> p a n h l", a=CHUNK, h=2, l=2),
+                    in0=x1_spread[:, 4 * P * t : 4 * P * (t + 1)]
+                    .rearrange("p (n h l) -> p n h l", h=2, l=2).unsqueeze(1).to_broadcast(shape),
+                    in1=bank[:].rearrange("p a n -> p (a n)").bitcast(BF16)
+                    .rearrange("p (a n l) -> p a n l", a=CHUNK, l=2).unsqueeze(3).to_broadcast(shape),
+                    op=MULT,
+                )
+                return
+            words = rows_n[step][:].bitcast(F32)
+            grouped_words = grouped[:].bitcast(F32).rearrange("p (a n u) -> p a n u", a=CHUNK, u=2)
+            for half in range(CHUNK // 2):
+                bank = turn.tile([P, 2, 2, P], F32, tag="bank")
+                for a in range(2):
+                    for u in range(2):
+                        first = P * (4 * half + 2 * a + u)
+                        nc.tensor.transpose(bank[:, a, u, :], words[:, first : first + P], ident_f[:])
+                nc.scalar.copy(
+                    out=grouped_words[:, 2 * half : 2 * half + 2, :, :],
+                    in_=bank[:].rearrange("p a u n -> p a n u"),
+                )
+
+        def quantise(step):
+            codes = stage.tile([P, CHUNK * P], U32, name="z_codes", align_bytes=64)
+            scales = stage.tile([P, CHUNK * P], U8, name="z_scales", align_bytes=64)
+            z_codes[step], z_scales[step] = codes, scales
+            nc.vector.quantize_mx(out=codes[:].bitcast(FP8X4), scales=scales[:], in_=z_grouped[step][:])
+
+        def multiply(step):
+            layer, t, c = chunks[step]
+            if c == 0:
+                acc[(layer, t)] = sums.tile([P, S], F32, name="acc")
+            group = acc[(layer, t)]
+            for a in range(CHUNK):
+                g = CHUNK * c + a
+                nc.tensor.matmul_mx(
+                    out=group[:],
+                    lhsT=z_codes[step][:, P * a : P * (a + 1)].bitcast(FP8X4),
+                    lhsT_scale=z_scales[step][:, P * a : P * (a + 1)],
+                    rhs=w_codes[layer][:, g, :].bitcast(FP8X4),
+                    rhs_scale=w_scales[layer][:, g, :],
+                    start=(g == 0),
+                    stop=(g == PASSES - 1),
+                )
+            if c < CHUNKS - 1:
+                return
+            if layer == 0:
+                o12[t] = stage.tile([P, LAYERS * S], F32, name="o12", bufs=4)
+                nc.vector.tensor_tensor(
+                    out=o12[t][:, 0:S].rearrange("p (u r e) -> p u r e", u=2, e=2),
+                    in0=group[:].rearrange("p (r u e) -> p u r e", u=2, e=2),
+                    in1=b1_rows[:].rearrange("p (u r e) -> p u r e", u=2, e=2),
+                    op=ADD,
+                )
+            else:
+                nc.scalar.copy(out=o12[t][:, S : 2 * S], in_=group[:])
+                window = pool_first - B_TILE * t
+                nc.tensor.matmul(
+                    out=pooled[:],
+                    lhsT=pool_sel[:, window : window + P],
+                    rhs=o12[t][:],
+                    start=(t == 0),
+                    stop=(t == N_TILES - 1),
+                )
+
+        for step in range(len(chunks) + 3):
+            if step < len(chunks):
+                start_chunk(step)
+            if step < CHUNKS:
+                prepare_weights(0, CHUNK * step, 2, nc.scalar.copy)
+                prepare_weights(0, CHUNK * step + 2, 2, nc.vector.tensor_copy)
+            elif step < 3 * CHUNKS:
+                prepare_weights(1, 2 * (step - CHUNKS), 2, nc.scalar.copy)
+            if step % (4 * CHUNKS) == LEAD and step // (4 * CHUNKS) < 3:
+                turn_x1(step // (4 * CHUNKS) + 1)
+            if 0 <= step - 1 < len(chunks):
+                turn_to_k(step - 1)
+            if 0 <= step - 2 < len(chunks):
+                quantise(step - 2)
+            if 0 <= step - 3 < len(chunks):
+                multiply(step - 3)
+
+        result = keep.tile([P, LAYERS * S], F32)
+        nc.vector.tensor_copy(
+            out=result[:, 0:S].rearrange("p (r u e) -> p u r e", u=2, e=2),
+            in_=pooled[:, 0:S].rearrange("p (u r e) -> p u r e", u=2, e=2),
+        )
+        nc.vector.tensor_tensor(out=result[:, S : 2 * S], in0=pooled[:, S : 2 * S], in1=late_bias[:], op=ADD)
+        nc.sync.dma_start(out=out[:, :], in_=result[0:B, :])

@@ -28,8 +28,12 @@ LAYERS = 2
 QUADS = 4
 QUAD = P // QUADS
 LEAD = 6
-SCALAR_EVERY_BESIDE = 2
-SCALAR_EVERY_ALONE = 4
+QUARTERS = 4
+B_QUARTER = B // QUARTERS
+N_QUARTER = N // QUARTERS
+SCALAR_BESIDE = 10
+SCALAR_ALONE = 4
+PINNED = {mybir.EngineType.PE, mybir.EngineType.Activation, mybir.EngineType.DVE}
 
 FLOPS = LAYERS * 2 * N * K * S
 
@@ -41,36 +45,93 @@ def tile_cin_pa_kernel(tc, x, x1, w1, b1, w2, b2, out):
         stage = stack.enter_context(tc.tile_pool(name="stage", bufs=3))
 
         x_fields = keep.tile([P, N // 2], BF16)
-        for h in range(2):
+        x_twice = keep.tile([P, N // 2, 2], BF16)
+
+        def load_x(quarter):
+            h, w = divmod(quarter, 2)
             nc.sync.dma_start(
-                out=x_fields[F0 * h : F0 * (h + 1), :].rearrange("i (b d) -> i b d", d=D),
-                in_=x[B // 2 * h : B // 2 * (h + 1)].rearrange("b i d -> i b d"),
+                out=x_fields[F0 * h : F0 * (h + 1), N_QUARTER * w : N_QUARTER * (w + 1)].rearrange(
+                    "i (b d) -> i b d", d=D
+                ),
+                in_=x[B_QUARTER * quarter : B_QUARTER * (quarter + 1)].rearrange("b i d -> i b d"),
             )
-        x1_fields = keep.tile([P, N], BF16)
+
+        def double_x(quarter):
+            h, w = divmod(quarter, 2)
+            rows, cols = slice(F0 * h, F0 * (h + 1)), slice(N_QUARTER * w, N_QUARTER * (w + 1))
+            nc.vector.tensor_copy(
+                out=x_twice[rows, cols, :],
+                in_=x_fields[rows, cols].unsqueeze(2).to_broadcast([F0, N_QUARTER, 2]),
+            )
+
+        x_spread = [keep.tile([P, PASSES, P, 2], BF16, name="x_spread%d" % t) for t in range(N_TILES)]
+
+        def park_x(quarter):
+            h, w = divmod(quarter, 2)
+            nc.sync.dma_start(
+                out=out[:, :],
+                in_=x_twice[F0 * h : F0 * (h + 1), N_QUARTER * w : N_QUARTER * (w + 1), :]
+                .rearrange("i n l -> i (n l)").bitcast(F32),
+            )
+
+        def spread_x(t, first, count):
+            parked = out.rearrange("(a q) (m n) -> q m a n", q=QUADS, m=2)[:, t % 2]
+            words = x_spread[t][:].rearrange("p a n l -> p (a n l)").bitcast(F32).rearrange(
+                "p (a n) -> p a n", a=PASSES
+            )
+            for q in range(QUADS):
+                nc.sync.dma_start(
+                    out=words[QUAD * q : QUAD * (q + 1), first : first + count, :],
+                    in_=parked[q, first : first + count, :].partition_broadcast(QUAD),
+                )
+
+        x1_rows = keep.tile([P, B, 4, D], BF16)
+        x1_spread = keep.tile([P, N, 4], BF16)
 
         def load_x1(quarter):
-            nc.sync.dma_start(
-                out=x1_fields[:, N // 4 * quarter : N // 4 * (quarter + 1)].rearrange("j (b d) -> j b d", d=D),
-                in_=x1[B // 4 * quarter : B // 4 * (quarter + 1)].rearrange("b j d -> j b d"),
+            samples = slice(B_QUARTER * quarter, B_QUARTER * (quarter + 1))
+            for q in range(QUADS):
+                nc.sync.dma_start(
+                    out=x1_rows[QUAD * q : QUAD * (q + 1), samples, :, :].rearrange("r b t d -> r b (t d)"),
+                    in_=x1[samples].rearrange("b (r t) d -> r b (t d)", t=4),
+                )
+
+        def group_x1(quarter, copy):
+            samples = slice(B_QUARTER * quarter, B_QUARTER * (quarter + 1))
+            copy(
+                out=x1_spread[:].rearrange("p (b d) t -> p b d t", d=D)[:, samples, :, :],
+                in_=x1_rows[:, samples, :, :].rearrange("p b t d -> p b d t"),
             )
 
         w_rows = [keep.tile([P, PASSES, 4, S], BF16, name="w_rows%d" % l) for l in range(LAYERS)]
 
-        def load_weights(layer):
-            source = (w1, w2)[layer].rearrange("(c g p t) s -> p c g (t s)", c=CHUNKS, p=P, t=4)
-            for c in range(CHUNKS):
-                rows = w_rows[layer][:, CHUNK * c : CHUNK * (c + 1), :, :]
-                nc.sync.dma_start(out=rows.rearrange("p g t s -> p g (t s)"), in_=source[:, c, :, :])
+        def load_weights(layer, c):
+            nc.sync.dma_start(
+                out=w_rows[layer][:, CHUNK * c : CHUNK * (c + 1), :, :].rearrange("p g t s -> p g (t s)"),
+                in_=(w1, w2)[layer].rearrange("(c g p t) s -> p c g (t s)", c=CHUNKS, p=P, t=4)[:, c, :, :],
+            )
 
-        load_x1(0)
         bias_bf = keep.tile([P, LAYERS, S], BF16)
+        load_x(0)
+        load_x1(0)
+        load_weights(0, 0)
+        double_x(0)
+        park_x(0)
+        load_weights(0, 1)
+        spread_x(0, 0, CHUNK)
+        load_weights(0, 2)
+        spread_x(0, CHUNK, PASSES - CHUNK)
+        load_weights(0, 3)
+        for quarter in range(1, QUARTERS):
+            load_x(quarter)
+        load_weights(1, 0)
+        spread_x(1, 0, PASSES)
+        for c in range(1, CHUNKS):
+            load_weights(1, c)
         nc.sync.dma_start(out=bias_bf[:, 0, :], in_=b1.partition_broadcast(P))
         nc.sync.dma_start(out=bias_bf[:, 1, :], in_=b2.partition_broadcast(P))
-        load_weights(0)
-        load_x1(1)
-        load_weights(1)
-        load_x1(2)
-        load_x1(3)
+        for quarter in range(1, QUARTERS):
+            load_x1(quarter)
 
         ident_bf = keep.tile([P, P], BF16)
         make_identity(nc, ident_bf[:])
@@ -85,129 +146,87 @@ def tile_cin_pa_kernel(tc, x, x1, w1, b1, w2, b2, out):
             axis=mybir.AxisListType.X,
             op=ADD,
         )
-        b1_rows = keep.tile([P, S], F32)
-        nc.vector.tensor_copy(
-            out=b1_rows[:].rearrange("p (u r e) -> p u r e", u=2, e=2),
-            in_=bias_bf[:, 0, :].rearrange("p (r u e) -> p u r e", u=2, e=2),
-        )
-        late_bias = keep.tile([P, S], F32)
-        nc.vector.tensor_scalar(out=late_bias[:], in0=bias_bf[:, 1, :], scalar1=float(D), scalar2=None, op0=MULT)
-
-        x_scalar = keep.tile([P, 4, 2, F0], F32)
-        x_pairs = keep.tile([P, 4, 2, F0, 2], BF16)
-        x1_spread = keep.tile([P, N_TILES * P * 4], BF16)
-        x1_spread_words = x1_spread[:].bitcast(F32).rearrange("p (a n h) -> p a n h", a=N_TILES, h=2)
         turn = stack.enter_context(tc.psum_pool(name="turn", bufs=4))
-        x_t = turn.tile([P, 4, P], BF16, tag="bank")
-        for m in range(4):
-            nc.tensor.transpose(x_t[:, m, :], x_fields[:, P * m : P * (m + 1)], ident_bf[:])
-        x_flat = x_t[:].rearrange("p m c -> p (m c)")
-        nc.vector.tensor_copy(out=x_scalar[:].rearrange("p m h i -> p (m h i)"), in_=x_flat)
-        nc.scalar.copy(
-            out=x_pairs[:].rearrange("p m h i r -> p (m h i) r"),
-            in_=x_flat.unsqueeze(2).to_broadcast([P, 4 * P, 2]),
-        )
-
-        def turn_x1(quarter):
-            x1_t = turn.tile([P, 2, P], BF16, tag="bank")
-            x1_copies = stage.tile([P, 2, 2, QUADS, QUAD], F32)
-            for a in range(2):
-                t = 2 * quarter + a
-                nc.tensor.transpose(x1_t[:, a, :], x1_fields[:, P * t : P * (t + 1)], ident_bf[:])
-            for a in range(2):
-                nc.scalar.copy(
-                    out=x1_copies[:, a, :, :, :],
-                    in_=x1_t[:, a, :].bitcast(F32).rearrange("p (r h) -> p h r", h=2).unsqueeze(2)
-                    .to_broadcast([P, 2, QUADS, QUAD]),
-                )
-            bank = turn.tile([P, 2, 2, P], F32, tag="bank")
-            for a in range(2):
-                for h in range(2):
-                    nc.tensor.transpose(
-                        bank[:, a, h, :], x1_copies[:, a, h, :, :].rearrange("p q r -> p (q r)"), ident_f[:]
-                    )
-            nc.scalar.copy(
-                out=x1_spread_words[:, 2 * quarter : 2 * quarter + 2, :, :],
-                in_=bank[:].rearrange("p a h n -> p a n h"),
-            )
-
-        turn_x1(0)
-
         sums = stack.enter_context(tc.psum_pool(name="sums", bufs=3))
         total = stack.enter_context(tc.psum_pool(name="total", bufs=1))
+
+        x_scalar = keep.tile([P, 4, 2, F0], F32)
+
+        def turn_x():
+            x_t = turn.tile([P, 4, P], BF16, tag="bank")
+            for m in range(4):
+                nc.tensor.transpose(x_t[:, m, :], x_fields[:, P * m : P * (m + 1)], ident_bf[:])
+            nc.scalar.copy(out=x_scalar[:].rearrange("p m h i -> p (m h i)"), in_=x_t[:].rearrange("p m c -> p (m c)"))
+
+        b1_rows = keep.tile([P, S], F32)
+        late_bias = keep.tile([P, S], F32)
+
+        def prepare_biases():
+            nc.vector.tensor_copy(
+                out=b1_rows[:].rearrange("p (u r e) -> p u r e", u=2, e=2),
+                in_=bias_bf[:, 0, :].rearrange("p (r u e) -> p u r e", u=2, e=2),
+            )
+            nc.vector.tensor_scalar(
+                out=late_bias[:], in0=bias_bf[:, 1, :], scalar1=float(D), scalar2=None, op0=MULT
+            )
 
         w_codes = [keep.tile([P, PASSES, S], U32, name="w_codes%d" % l, align_bytes=64) for l in range(LAYERS)]
         w_scales = [keep.tile([P, PASSES, S], U8, name="w_scales%d" % l, align_bytes=64) for l in range(LAYERS)]
         pooled = total.tile([P, LAYERS * S], F32)
 
-        def prepare_weights(layer, first, count, copy):
-            w_grouped = stage.tile([P, count, S, 4], BF16, align_bytes=64, tag="w_grouped%d" % count)
-            copy(
-                out=w_grouped[:],
-                in_=w_rows[layer][:, first : first + count, :, :].rearrange("p g t s -> p g s t"),
-            )
-            nc.vector.quantize_mx(
-                out=w_codes[layer][:, first : first + count, :].rearrange("p g s -> p (g s)").bitcast(FP8X4),
-                scales=w_scales[layer][:, first : first + count, :].rearrange("p g s -> p (g s)"),
-                in_=w_grouped[:].rearrange("p g s t -> p (g s t)"),
-            )
+        w_grouped = {}
 
-        per_layer = [[(layer, t, c) for t in range(N_TILES) for c in range(CHUNKS)] for layer in range(LAYERS)]
-        chunks = []
-        for k in range(N_TILES * CHUNKS + LEAD):
-            if k < N_TILES * CHUNKS:
-                chunks.append(per_layer[0][k])
-            if k >= LEAD:
-                chunks.append(per_layer[1][k - LEAD])
-        last_of_layer_1 = chunks.index(per_layer[0][-1])
+        def group_weights(layer, c, copies):
+            w_grouped[(layer, c)] = stage.tile([P, CHUNK, S, 4], BF16, align_bytes=64, name="w_grouped")
+            for half, copy in enumerate(copies):
+                copy(
+                    out=w_grouped[(layer, c)][:, 2 * half : 2 * half + 2, :, :],
+                    in_=w_rows[layer][:, CHUNK * c + 2 * half : CHUNK * c + 2 * half + 2, :, :]
+                    .rearrange("p g t s -> p g s t"),
+                )
+
+        def quantise_weights(layer, c):
+            chunk = slice(CHUNK * c, CHUNK * (c + 1))
+            nc.vector.quantize_mx(
+                out=w_codes[layer][:, chunk, :].rearrange("p g s -> p (g s)").bitcast(FP8X4),
+                scales=w_scales[layer][:, chunk, :].rearrange("p g s -> p (g s)"),
+                in_=w_grouped[(layer, c)][:].rearrange("p g s t -> p (g s t)"),
+            )
 
         rows_n, z_grouped, z_codes, z_scales, acc, o12 = {}, {}, {}, {}, {}, {}
 
-        def start_chunk(step):
-            layer, t, c = chunks[step]
-            m, h = t % 4, t // 4
-            first_i = I_CHUNK * c
-            if layer == 0:
-                x_copies = stage.tile([P, CHUNK, QUADS, QUAD], F32)
-                rows_n[step] = x_copies
-                words = x_pairs[:, m, h, first_i : first_i + I_CHUNK, :].rearrange("p i r -> p (i r)").bitcast(F32)
-                nc.scalar.copy(
-                    out=x_copies[:],
-                    in_=words.rearrange("p (a q) -> p a q", q=QUADS).unsqueeze(3).to_broadcast([P, CHUNK, QUADS, QUAD]),
-                )
-                return
+        def form_z1(j):
+            t, c = divmod(j, CHUNKS)
+            grouped = stage.tile([P, CHUNK * P * 4], BF16, name="z_grouped", align_bytes=64, bufs=5)
+            z_grouped[(0, j)] = grouped
+            shape = [P, CHUNK * P, 2, 2]
+            nc.vector.tensor_tensor(
+                out=grouped[:].rearrange("p (a w) -> p a w", a=CHUNK),
+                in0=x1_spread[:, P * t : P * (t + 1), :].rearrange("p n t -> p (n t)")
+                .unsqueeze(1).to_broadcast([P, CHUNK, 4 * P]),
+                in1=x_spread[t][:, CHUNK * c : CHUNK * (c + 1), :, :].rearrange("p a n l -> p (a n) l")
+                .unsqueeze(2).to_broadcast(shape),
+                op=MULT,
+            )
+
+        def form_z2(j, on_scalar):
+            t, c = divmod(j, CHUNKS)
             z = stage.tile([P, I_CHUNK * FK], BF16, name="z_rows")
-            rows_n[step] = z
-            every = SCALAR_EVERY_BESIDE if step < last_of_layer_1 else SCALAR_EVERY_ALONE
+            rows_n[j] = z
             for i in range(I_CHUNK):
-                x_i = x_scalar[:, m, h, first_i + i : first_i + i + 1]
+                x_i = x_scalar[:, t % 4, t // 4, I_CHUNK * c + i : I_CHUNK * c + i + 1]
                 a, q = divmod(i, I_PASS)
                 z_i = z[:, K_PASS * a : K_PASS * (a + 1)].rearrange("p (u q w) -> p u q w", u=2, q=I_PASS)[:, :, q, :]
                 o1_t = o12[t][:, 0:S].rearrange("p (u w) -> p u w", u=2)
-                if i % every == every - 1:
+                if i * on_scalar % I_CHUNK < on_scalar:
                     nc.scalar.activation(out=z_i, in_=o1_t, func=COPY, scale=x_i)
                 else:
                     nc.vector.tensor_scalar(out=z_i, in0=o1_t, scalar1=x_i, scalar2=None, op0=MULT)
 
-        def turn_to_k(step):
-            layer, t, c = chunks[step]
-            grouped = stage.tile([P, CHUNK * P * 4], BF16, name="z_grouped", align_bytes=64)
-            z_grouped[step] = grouped
-            if layer == 0:
-                bank = turn.tile([P, CHUNK, P], F32, tag="bank")
-                for a in range(CHUNK):
-                    nc.tensor.transpose(bank[:, a, :], rows_n[step][:, a, :, :].rearrange("p q r -> p (q r)"), ident_f[:])
-                shape = [P, CHUNK, P, 2, 2]
-                nc.vector.tensor_tensor(
-                    out=grouped[:].rearrange("p (a n h l) -> p a n h l", a=CHUNK, h=2, l=2),
-                    in0=x1_spread[:, 4 * P * t : 4 * P * (t + 1)]
-                    .rearrange("p (n h l) -> p n h l", h=2, l=2).unsqueeze(1).to_broadcast(shape),
-                    in1=bank[:].rearrange("p a n -> p (a n)").bitcast(BF16)
-                    .rearrange("p (a n l) -> p a n l", a=CHUNK, l=2).unsqueeze(3).to_broadcast(shape),
-                    op=MULT,
-                )
-                return
-            words = rows_n[step][:].bitcast(F32)
+        def turn_z2(j):
+            grouped = stage.tile([P, CHUNK * P * 4], BF16, name="z_grouped", align_bytes=64, bufs=5)
+            z_grouped[(1, j)] = grouped
+            words = rows_n[j][:].bitcast(F32)
             grouped_words = grouped[:].bitcast(F32).rearrange("p (a n u) -> p a n u", a=CHUNK, u=2)
             for half in range(CHUNK // 2):
                 bank = turn.tile([P, 2, 2, P], F32, tag="bank")
@@ -220,65 +239,94 @@ def tile_cin_pa_kernel(tc, x, x1, w1, b1, w2, b2, out):
                     in_=bank[:].rearrange("p a u n -> p a n u"),
                 )
 
-        def quantise(step):
-            codes = stage.tile([P, CHUNK * P], U32, name="z_codes", align_bytes=64)
-            scales = stage.tile([P, CHUNK * P], U8, name="z_scales", align_bytes=64)
-            z_codes[step], z_scales[step] = codes, scales
-            nc.vector.quantize_mx(out=codes[:].bitcast(FP8X4), scales=scales[:], in_=z_grouped[step][:])
+        def quantise(layer, j):
+            codes = stage.tile([P, CHUNK * P], U32, name="z_codes", align_bytes=64, bufs=5)
+            scales = stage.tile([P, CHUNK * P], U8, name="z_scales", align_bytes=64, bufs=5)
+            z_codes[(layer, j)], z_scales[(layer, j)] = codes, scales
+            nc.vector.quantize_mx(out=codes[:].bitcast(FP8X4), scales=scales[:], in_=z_grouped[(layer, j)][:])
 
-        def multiply(step):
-            layer, t, c = chunks[step]
+        def multiply(layer, j):
+            t, c = divmod(j, CHUNKS)
             if c == 0:
                 acc[(layer, t)] = sums.tile([P, S], F32, name="acc")
-            group = acc[(layer, t)]
             for a in range(CHUNK):
                 g = CHUNK * c + a
                 nc.tensor.matmul_mx(
-                    out=group[:],
-                    lhsT=z_codes[step][:, P * a : P * (a + 1)].bitcast(FP8X4),
-                    lhsT_scale=z_scales[step][:, P * a : P * (a + 1)],
+                    out=acc[(layer, t)][:],
+                    lhsT=z_codes[(layer, j)][:, P * a : P * (a + 1)].bitcast(FP8X4),
+                    lhsT_scale=z_scales[(layer, j)][:, P * a : P * (a + 1)],
                     rhs=w_codes[layer][:, g, :].bitcast(FP8X4),
                     rhs_scale=w_scales[layer][:, g, :],
                     start=(g == 0),
                     stop=(g == PASSES - 1),
                 )
-            if c < CHUNKS - 1:
-                return
-            if layer == 0:
-                o12[t] = stage.tile([P, LAYERS * S], F32, name="o12", bufs=4)
-                nc.vector.tensor_tensor(
-                    out=o12[t][:, 0:S].rearrange("p (u r e) -> p u r e", u=2, e=2),
-                    in0=group[:].rearrange("p (r u e) -> p u r e", u=2, e=2),
-                    in1=b1_rows[:].rearrange("p (u r e) -> p u r e", u=2, e=2),
-                    op=ADD,
-                )
-            else:
-                nc.scalar.copy(out=o12[t][:, S : 2 * S], in_=group[:])
-                window = pool_first - B_TILE * t
-                nc.tensor.matmul(
-                    out=pooled[:],
-                    lhsT=pool_sel[:, window : window + P],
-                    rhs=o12[t][:],
-                    start=(t == 0),
-                    stop=(t == N_TILES - 1),
-                )
 
-        for step in range(len(chunks) + 3):
-            if step < len(chunks):
-                start_chunk(step)
-            if step < CHUNKS:
-                prepare_weights(0, CHUNK * step, 2, nc.scalar.copy)
-                prepare_weights(0, CHUNK * step + 2, 2, nc.vector.tensor_copy)
-            elif step < 3 * CHUNKS:
-                prepare_weights(1, 2 * (step - CHUNKS), 2, nc.scalar.copy)
-            if step % (4 * CHUNKS) == LEAD and step // (4 * CHUNKS) < 3:
-                turn_x1(step // (4 * CHUNKS) + 1)
-            if 0 <= step - 1 < len(chunks):
-                turn_to_k(step - 1)
-            if 0 <= step - 2 < len(chunks):
-                quantise(step - 2)
-            if 0 <= step - 3 < len(chunks):
-                multiply(step - 3)
+        def finish_o1(t):
+            o12[t] = stage.tile([P, LAYERS * S], F32, name="o12", bufs=4)
+            nc.vector.tensor_tensor(
+                out=o12[t][:, 0:S].rearrange("p (u r e) -> p u r e", u=2, e=2),
+                in0=acc[(0, t)][:].rearrange("p (r u e) -> p u r e", u=2, e=2),
+                in1=b1_rows[:].rearrange("p (u r e) -> p u r e", u=2, e=2),
+                op=ADD,
+            )
+
+        def finish_o2(t):
+            nc.scalar.copy(out=o12[t][:, S : 2 * S], in_=acc[(1, t)][:])
+
+        def pool_rows(t):
+            window = pool_first - B_TILE * t
+            nc.tensor.matmul(
+                out=pooled[:],
+                lhsT=pool_sel[:, window : window + P],
+                rhs=o12[t][:],
+                start=(t == 0),
+                stop=(t == N_TILES - 1),
+            )
+
+        halves = (nc.scalar.copy, nc.vector.tensor_copy)
+        group_x1(0, nc.scalar.copy)
+        for c in range(CHUNKS):
+            group_weights(0, c, halves)
+            quantise_weights(0, c)
+        n_chunks = N_TILES * CHUNKS
+        stack.enter_context(tc.manual_schedule(engines=PINNED))
+        for r in range(n_chunks + LEAD + 4):
+            k = r - LEAD
+            if 0 <= r - 1 < CHUNKS:
+                group_weights(1, r - 1, [nc.scalar.copy] * 2)
+            if 0 <= r - 4 < CHUNKS:
+                quantise_weights(1, r - 4)
+            if r == 5:
+                turn_x()
+                prepare_biases()
+            if 0 <= r - 2 < n_chunks:
+                multiply(0, r - 2)
+            if 0 <= k < n_chunks:
+                form_z2(k, SCALAR_BESIDE if r < n_chunks else SCALAR_ALONE)
+            if 0 <= k - 4 < n_chunks and (k - 4) % CHUNKS == CHUNKS - 1:
+                finish_o2((k - 4) // CHUNKS)
+            if r < n_chunks:
+                form_z1(r)
+            if 0 <= r - 2 < n_chunks and (r - 2) % CHUNKS == CHUNKS - 1:
+                finish_o1((r - 2) // CHUNKS)
+            if 0 <= k - 1 < n_chunks:
+                turn_z2(k - 1)
+            if 0 <= r - 1 < n_chunks:
+                quantise(0, r - 1)
+            if 0 <= k - 2 < n_chunks:
+                quantise(1, k - 2)
+            if 0 <= k - 3 < n_chunks:
+                multiply(1, k - 3)
+            if 0 <= k - 4 < n_chunks and (k - 4) % CHUNKS == CHUNKS - 1:
+                pool_rows((k - 4) // CHUNKS)
+            if r in (1, 6, 14):
+                quarter = (1, 6, 14).index(r) + 1
+                double_x(quarter)
+                park_x(quarter)
+                spread_x(2 * quarter, 0, PASSES)
+                spread_x(2 * quarter + 1, 0, PASSES)
+            if r in (5, 10, 18):
+                group_x1((5, 10, 18).index(r) + 1, nc.scalar.copy)
 
         result = keep.tile([P, LAYERS * S], F32)
         nc.vector.tensor_copy(

@@ -31,8 +31,9 @@ LEAD = 6
 QUARTERS = 4
 B_QUARTER = B // QUARTERS
 N_QUARTER = N // QUARTERS
-SCALAR_BESIDE = 10
+SCALAR_BESIDE = 11
 SCALAR_ALONE = 4
+FIRST_SPREAD = 2
 PINNED = {mybir.EngineType.PE, mybir.EngineType.Activation, mybir.EngineType.DVE}
 
 FLOPS = LAYERS * 2 * N * K * S
@@ -47,42 +48,37 @@ def tile_cin_pa_kernel(tc, x, x1, w1, b1, w2, b2, out):
         x_fields = keep.tile([P, N // 2], BF16)
         x_twice = keep.tile([P, N // 2, 2], BF16)
 
-        def load_x(quarter):
-            h, w = divmod(quarter, 2)
-            nc.sync.dma_start(
-                out=x_fields[F0 * h : F0 * (h + 1), N_QUARTER * w : N_QUARTER * (w + 1)].rearrange(
-                    "i (b d) -> i b d", d=D
-                ),
-                in_=x[B_QUARTER * quarter : B_QUARTER * (quarter + 1)].rearrange("b i d -> i b d"),
-            )
+        def load_x(h):
+            samples = x[B // 2 * h : B // 2 * (h + 1)].rearrange("b (a q) d -> q a b d", q=QUADS)
+            for q in range(QUADS):
+                first = F0 * h + PASSES * q
+                nc.sync.dma_start(
+                    out=x_fields[first : first + PASSES, :].rearrange("a (b d) -> a b d", d=D), in_=samples[q]
+                )
 
-        def double_x(quarter):
-            h, w = divmod(quarter, 2)
-            rows, cols = slice(F0 * h, F0 * (h + 1)), slice(N_QUARTER * w, N_QUARTER * (w + 1))
+        def double_x(w):
+            cols = slice(N_QUARTER * w, N_QUARTER * (w + 1))
             nc.vector.tensor_copy(
-                out=x_twice[rows, cols, :],
-                in_=x_fields[rows, cols].unsqueeze(2).to_broadcast([F0, N_QUARTER, 2]),
+                out=x_twice[:, cols, :], in_=x_fields[:, cols].unsqueeze(2).to_broadcast([P, N_QUARTER, 2])
             )
 
-        x_spread = [keep.tile([P, PASSES, P, 2], BF16, name="x_spread%d" % t) for t in range(N_TILES)]
+        x_spread = [keep.tile([P, PASSES, P, 2], BF16, name="x_spread%d" % t) for t in range(FIRST_SPREAD, N_TILES)]
 
-        def park_x(quarter):
-            h, w = divmod(quarter, 2)
+        def park_x(t):
+            h, m = divmod(t, 4)
+            half = out[B // 2 * (t % 2) : B // 2 * (t % 2 + 1), :]
             nc.sync.dma_start(
-                out=out[:, :],
-                in_=x_twice[F0 * h : F0 * (h + 1), N_QUARTER * w : N_QUARTER * (w + 1), :]
-                .rearrange("i n l -> i (n l)").bitcast(F32),
+                out=half.rearrange("r (u n) -> (r u) n", n=P),
+                in_=x_twice[F0 * h : F0 * (h + 1), P * m : P * (m + 1), :].rearrange("i n l -> i (n l)").bitcast(F32),
             )
 
-        def spread_x(t, first, count):
-            parked = out.rearrange("(a q) (m n) -> q m a n", q=QUADS, m=2)[:, t % 2]
-            words = x_spread[t][:].rearrange("p a n l -> p (a n l)").bitcast(F32).rearrange(
-                "p (a n) -> p a n", a=PASSES
-            )
+        def spread_x(t):
+            half = out[B // 2 * (t % 2) : B // 2 * (t % 2 + 1), :]
+            parked = half.rearrange("(q r) n -> q (r n)", q=QUADS)
+            words = x_spread[t - FIRST_SPREAD][:].rearrange("p a n l -> p (a n l)").bitcast(F32)
             for q in range(QUADS):
                 nc.sync.dma_start(
-                    out=words[QUAD * q : QUAD * (q + 1), first : first + count, :],
-                    in_=parked[q, first : first + count, :].partition_broadcast(QUAD),
+                    out=words[QUAD * q : QUAD * (q + 1), :], in_=parked[q].partition_broadcast(QUAD)
                 )
 
         x1_rows = keep.tile([P, B, 4, D], BF16)
@@ -113,25 +109,15 @@ def tile_cin_pa_kernel(tc, x, x1, w1, b1, w2, b2, out):
 
         bias_bf = keep.tile([P, LAYERS, S], BF16)
         load_x(0)
-        load_x1(0)
+        load_x(1)
         load_weights(0, 0)
-        double_x(0)
-        park_x(0)
-        load_weights(0, 1)
-        spread_x(0, 0, CHUNK)
-        load_weights(0, 2)
-        spread_x(0, CHUNK, PASSES - CHUNK)
-        load_weights(0, 3)
-        for quarter in range(1, QUARTERS):
-            load_x(quarter)
-        load_weights(1, 0)
-        spread_x(1, 0, PASSES)
+        load_x1(0)
         for c in range(1, CHUNKS):
-            load_weights(1, c)
+            load_weights(0, c)
         nc.sync.dma_start(out=bias_bf[:, 0, :], in_=b1.partition_broadcast(P))
         nc.sync.dma_start(out=bias_bf[:, 1, :], in_=b2.partition_broadcast(P))
-        for quarter in range(1, QUARTERS):
-            load_x1(quarter)
+        load_weights(1, 0)
+        load_weights(1, 1)
 
         ident_bf = keep.tile([P, P], BF16)
         make_identity(nc, ident_bf[:])
@@ -150,13 +136,24 @@ def tile_cin_pa_kernel(tc, x, x1, w1, b1, w2, b2, out):
         sums = stack.enter_context(tc.psum_pool(name="sums", bufs=3))
         total = stack.enter_context(tc.psum_pool(name="total", bufs=1))
 
-        x_scalar = keep.tile([P, 4, 2, F0], F32)
+        x_scalar = keep.tile([P, 4, 2, QUADS, PASSES], F32)
 
         def turn_x():
             x_t = turn.tile([P, 4, P], BF16, tag="bank")
             for m in range(4):
                 nc.tensor.transpose(x_t[:, m, :], x_fields[:, P * m : P * (m + 1)], ident_bf[:])
-            nc.scalar.copy(out=x_scalar[:].rearrange("p m h i -> p (m h i)"), in_=x_t[:].rearrange("p m c -> p (m c)"))
+            nc.scalar.copy(
+                out=x_scalar[:].rearrange("p m h q a -> p (m h q a)"), in_=x_t[:].rearrange("p m c -> p (m c)")
+            )
+
+        field_sel = keep.tile([P, PASSES, QUADS, QUAD], BF16)
+
+        def make_field_sel():
+            nc.vector.tensor_copy(
+                out=field_sel[:],
+                in_=ident_bf[:, 0:F0].rearrange("p (q a) -> p a q", q=QUADS).unsqueeze(3)
+                .to_broadcast([P, PASSES, QUADS, QUAD]),
+            )
 
         b1_rows = keep.tile([P, S], F32)
         late_bias = keep.tile([P, S], F32)
@@ -177,7 +174,7 @@ def tile_cin_pa_kernel(tc, x, x1, w1, b1, w2, b2, out):
         w_grouped = {}
 
         def group_weights(layer, c, copies):
-            w_grouped[(layer, c)] = stage.tile([P, CHUNK, S, 4], BF16, align_bytes=64, name="w_grouped")
+            w_grouped[(layer, c)] = stage.tile([P, CHUNK, S, 4], BF16, align_bytes=64, name="w_grouped", bufs=4)
             for half, copy in enumerate(copies):
                 copy(
                     out=w_grouped[(layer, c)][:, 2 * half : 2 * half + 2, :, :],
@@ -195,17 +192,34 @@ def tile_cin_pa_kernel(tc, x, x1, w1, b1, w2, b2, out):
 
         rows_n, z_grouped, z_codes, z_scales, acc, o12 = {}, {}, {}, {}, {}, {}
 
+        x_banks = {}
+
+        def select_x(j):
+            t, c = divmod(j, CHUNKS)
+            x_banks[j] = turn.tile([P, CHUNK, 2 * P], BF16, tag="bank", name="x_bank")
+            for a in range(CHUNK):
+                nc.tensor.matmul(
+                    out=x_banks[j][:, a, :],
+                    lhsT=field_sel[:, CHUNK * c + a, :, :].rearrange("p q r -> p (q r)"),
+                    rhs=x_twice[:, P * t : P * (t + 1), :].rearrange("p n l -> p (n l)"),
+                    start=True,
+                    stop=True,
+                )
+
         def form_z1(j):
             t, c = divmod(j, CHUNKS)
             grouped = stage.tile([P, CHUNK * P * 4], BF16, name="z_grouped", align_bytes=64, bufs=5)
             z_grouped[(0, j)] = grouped
             shape = [P, CHUNK * P, 2, 2]
+            if t < FIRST_SPREAD:
+                x_words = x_banks[j][:].rearrange("p a (n l) -> p (a n) l", l=2)
+            else:
+                x_words = x_spread[t - FIRST_SPREAD][:, CHUNK * c : CHUNK * (c + 1), :, :].rearrange("p a n l -> p (a n) l")
             nc.vector.tensor_tensor(
                 out=grouped[:].rearrange("p (a w) -> p a w", a=CHUNK),
                 in0=x1_spread[:, P * t : P * (t + 1), :].rearrange("p n t -> p (n t)")
                 .unsqueeze(1).to_broadcast([P, CHUNK, 4 * P]),
-                in1=x_spread[t][:, CHUNK * c : CHUNK * (c + 1), :, :].rearrange("p a n l -> p (a n) l")
-                .unsqueeze(2).to_broadcast(shape),
+                in1=x_words.unsqueeze(2).to_broadcast(shape),
                 op=MULT,
             )
 
@@ -214,8 +228,8 @@ def tile_cin_pa_kernel(tc, x, x1, w1, b1, w2, b2, out):
             z = stage.tile([P, I_CHUNK * FK], BF16, name="z_rows")
             rows_n[j] = z
             for i in range(I_CHUNK):
-                x_i = x_scalar[:, t % 4, t // 4, I_CHUNK * c + i : I_CHUNK * c + i + 1]
                 a, q = divmod(i, I_PASS)
+                x_i = x_scalar[:, t % 4, t // 4, q, CHUNK * c + a : CHUNK * c + a + 1]
                 z_i = z[:, K_PASS * a : K_PASS * (a + 1)].rearrange("p (u q w) -> p u q w", u=2, q=I_PASS)[:, :, q, :]
                 o1_t = o12[t][:, 0:S].rearrange("p (u w) -> p u w", u=2)
                 if i * on_scalar % I_CHUNK < on_scalar:
@@ -283,22 +297,18 @@ def tile_cin_pa_kernel(tc, x, x1, w1, b1, w2, b2, out):
                 stop=(t == N_TILES - 1),
             )
 
-        halves = (nc.scalar.copy, nc.vector.tensor_copy)
-        group_x1(0, nc.scalar.copy)
-        for c in range(CHUNKS):
-            group_weights(0, c, halves)
-            quantise_weights(0, c)
+        on_scalar = [nc.scalar.copy] * 2
         n_chunks = N_TILES * CHUNKS
+        n_selected = FIRST_SPREAD * CHUNKS
         stack.enter_context(tc.manual_schedule(engines=PINNED))
+        make_field_sel()
+        double_x(0)
+        select_x(0)
+        turn_x()
+        group_weights(0, 0, [nc.vector.tensor_copy] * 2)
+        group_x1(0, nc.vector.tensor_copy)
         for r in range(n_chunks + LEAD + 4):
             k = r - LEAD
-            if 0 <= r - 1 < CHUNKS:
-                group_weights(1, r - 1, [nc.scalar.copy] * 2)
-            if 0 <= r - 4 < CHUNKS:
-                quantise_weights(1, r - 4)
-            if r == 5:
-                turn_x()
-                prepare_biases()
             if 0 <= r - 2 < n_chunks:
                 multiply(0, r - 2)
             if 0 <= k < n_chunks:
@@ -307,6 +317,18 @@ def tile_cin_pa_kernel(tc, x, x1, w1, b1, w2, b2, out):
                 finish_o2((k - 4) // CHUNKS)
             if r < n_chunks:
                 form_z1(r)
+            if r + 1 < n_selected:
+                select_x(r + 1)
+            if 1 <= r + 1 < CHUNKS:
+                group_weights(0, r + 1, on_scalar)
+            if 0 <= r - 3 < CHUNKS:
+                group_weights(1, r - 3, on_scalar)
+            if r < CHUNKS:
+                quantise_weights(0, r)
+            if 0 <= r - 4 < CHUNKS:
+                quantise_weights(1, r - 4)
+            if r == 3:
+                prepare_biases()
             if 0 <= r - 2 < n_chunks and (r - 2) % CHUNKS == CHUNKS - 1:
                 finish_o1((r - 2) // CHUNKS)
             if 0 <= k - 1 < n_chunks:
@@ -319,14 +341,19 @@ def tile_cin_pa_kernel(tc, x, x1, w1, b1, w2, b2, out):
                 multiply(1, k - 3)
             if 0 <= k - 4 < n_chunks and (k - 4) % CHUNKS == CHUNKS - 1:
                 pool_rows((k - 4) // CHUNKS)
-            if r in (1, 6, 14):
-                quarter = (1, 6, 14).index(r) + 1
-                double_x(quarter)
-                park_x(quarter)
-                spread_x(2 * quarter, 0, PASSES)
-                spread_x(2 * quarter + 1, 0, PASSES)
-            if r in (5, 10, 18):
-                group_x1((5, 10, 18).index(r) + 1, nc.scalar.copy)
+            if r in (1, 2, 6, 10, 14, 18):
+                t = (1, 2, 6, 10, 14, 18).index(r) + FIRST_SPREAD
+                if t == FIRST_SPREAD:
+                    double_x(1)
+                park_x(t)
+                spread_x(t)
+            if r == 1:
+                load_weights(1, 2)
+                load_weights(1, 3)
+            if r in (3, 10, 18):
+                load_x1((3, 10, 18).index(r) + 1)
+            if r in (7, 14, 22):
+                group_x1((7, 14, 22).index(r) + 1, nc.scalar.copy)
 
         result = keep.tile([P, LAYERS * S], F32)
         nc.vector.tensor_copy(

@@ -31,7 +31,7 @@ LEAD = 6
 QUARTERS = 4
 B_QUARTER = B // QUARTERS
 N_QUARTER = N // QUARTERS
-SCALAR_BESIDE = 11
+SCALAR_BESIDE = 10
 SCALAR_ALONE = 4
 FIRST_SPREAD = 2
 PINNED = {mybir.EngineType.PE, mybir.EngineType.Activation, mybir.EngineType.DVE}
@@ -110,9 +110,8 @@ def tile_cin_pa_kernel(tc, x, x1, w1, b1, w2, b2, out):
         bias_bf = keep.tile([P, LAYERS, S], BF16)
         load_x(0)
         load_x(1)
-        load_weights(0, 0)
         load_x1(0)
-        for c in range(1, CHUNKS):
+        for c in range(CHUNKS):
             load_weights(0, c)
         nc.sync.dma_start(out=bias_bf[:, 0, :], in_=b1.partition_broadcast(P))
         nc.sync.dma_start(out=bias_bf[:, 1, :], in_=b2.partition_broadcast(P))
@@ -169,7 +168,6 @@ def tile_cin_pa_kernel(tc, x, x1, w1, b1, w2, b2, out):
 
         w_codes = [keep.tile([P, PASSES, S], U32, name="w_codes%d" % l, align_bytes=64) for l in range(LAYERS)]
         w_scales = [keep.tile([P, PASSES, S], U8, name="w_scales%d" % l, align_bytes=64) for l in range(LAYERS)]
-        pooled = total.tile([P, LAYERS * S], F32)
 
         w_grouped = {}
 
@@ -190,7 +188,13 @@ def tile_cin_pa_kernel(tc, x, x1, w1, b1, w2, b2, out):
                 in_=w_grouped[(layer, c)][:].rearrange("p g s t -> p (g s t)"),
             )
 
-        rows_n, z_grouped, z_codes, z_scales, acc, o12 = {}, {}, {}, {}, {}, {}
+        rows_n, z_grouped, z_codes, z_scales, acc, o1, o2 = {}, {}, {}, {}, {}, {}, {}
+
+        def grouped_half(r, layer):
+            if r not in z_grouped:
+                z_grouped[r] = stage.tile([P, LAYERS, CHUNK * P * 4], BF16, name="z_grouped", align_bytes=64)
+            return z_grouped[r][:, layer, :]
+
 
         x_banks = {}
 
@@ -208,15 +212,14 @@ def tile_cin_pa_kernel(tc, x, x1, w1, b1, w2, b2, out):
 
         def form_z1(j):
             t, c = divmod(j, CHUNKS)
-            grouped = stage.tile([P, CHUNK * P * 4], BF16, name="z_grouped", align_bytes=64, bufs=5)
-            z_grouped[(0, j)] = grouped
+            grouped = grouped_half(j, 0)
             shape = [P, CHUNK * P, 2, 2]
             if t < FIRST_SPREAD:
                 x_words = x_banks[j][:].rearrange("p a (n l) -> p (a n) l", l=2)
             else:
                 x_words = x_spread[t - FIRST_SPREAD][:, CHUNK * c : CHUNK * (c + 1), :, :].rearrange("p a n l -> p (a n) l")
             nc.vector.tensor_tensor(
-                out=grouped[:].rearrange("p (a w) -> p a w", a=CHUNK),
+                out=grouped.rearrange("p (a w) -> p a w", a=CHUNK),
                 in0=x1_spread[:, P * t : P * (t + 1), :].rearrange("p n t -> p (n t)")
                 .unsqueeze(1).to_broadcast([P, CHUNK, 4 * P]),
                 in1=x_words.unsqueeze(2).to_broadcast(shape),
@@ -231,17 +234,16 @@ def tile_cin_pa_kernel(tc, x, x1, w1, b1, w2, b2, out):
                 a, q = divmod(i, I_PASS)
                 x_i = x_scalar[:, t % 4, t // 4, q, CHUNK * c + a : CHUNK * c + a + 1]
                 z_i = z[:, K_PASS * a : K_PASS * (a + 1)].rearrange("p (u q w) -> p u q w", u=2, q=I_PASS)[:, :, q, :]
-                o1_t = o12[t][:, 0:S].rearrange("p (u w) -> p u w", u=2)
+                o1_t = o1[t][:].rearrange("p (u w) -> p u w", u=2)
                 if i * on_scalar % I_CHUNK < on_scalar:
                     nc.scalar.activation(out=z_i, in_=o1_t, func=COPY, scale=x_i)
                 else:
                     nc.vector.tensor_scalar(out=z_i, in0=o1_t, scalar1=x_i, scalar2=None, op0=MULT)
 
-        def turn_z2(j):
-            grouped = stage.tile([P, CHUNK * P * 4], BF16, name="z_grouped", align_bytes=64, bufs=5)
-            z_grouped[(1, j)] = grouped
+        def turn_z2(j, r):
+            grouped = grouped_half(r, 1)
             words = rows_n[j][:].bitcast(F32)
-            grouped_words = grouped[:].bitcast(F32).rearrange("p (a n u) -> p a n u", a=CHUNK, u=2)
+            grouped_words = grouped.bitcast(F32).rearrange("p (a n u) -> p a n u", a=CHUNK, u=2)
             for half in range(CHUNK // 2):
                 bank = turn.tile([P, 2, 2, P], F32, tag="bank")
                 for a in range(2):
@@ -253,13 +255,19 @@ def tile_cin_pa_kernel(tc, x, x1, w1, b1, w2, b2, out):
                     in_=bank[:].rearrange("p a u n -> p a n u"),
                 )
 
-        def quantise(layer, j):
-            codes = stage.tile([P, CHUNK * P], U32, name="z_codes", align_bytes=64, bufs=5)
-            scales = stage.tile([P, CHUNK * P], U8, name="z_scales", align_bytes=64, bufs=5)
-            z_codes[(layer, j)], z_scales[(layer, j)] = codes, scales
-            nc.vector.quantize_mx(out=codes[:].bitcast(FP8X4), scales=scales[:], in_=z_grouped[(layer, j)][:])
+        def quantise(r):
+            first = 0 if r < n_chunks else 1
+            last = 1 if r - LEAD - 1 >= 0 else 0
+            codes = stage.tile([P, LAYERS, CHUNK * P], U32, name="z_codes", align_bytes=64)
+            scales = stage.tile([P, LAYERS, CHUNK * P], U8, name="z_scales", align_bytes=64)
+            z_codes[r], z_scales[r] = codes, scales
+            nc.vector.quantize_mx(
+                out=codes[:, first : last + 1, :].rearrange("p l w -> p (l w)").bitcast(FP8X4),
+                scales=scales[:, first : last + 1, :].rearrange("p l w -> p (l w)"),
+                in_=z_grouped[r][:, first : last + 1, :].rearrange("p l w -> p (l w)"),
+            )
 
-        def multiply(layer, j):
+        def multiply(layer, j, r):
             t, c = divmod(j, CHUNKS)
             if c == 0:
                 acc[(layer, t)] = sums.tile([P, S], F32, name="acc")
@@ -267,8 +275,8 @@ def tile_cin_pa_kernel(tc, x, x1, w1, b1, w2, b2, out):
                 g = CHUNK * c + a
                 nc.tensor.matmul_mx(
                     out=acc[(layer, t)][:],
-                    lhsT=z_codes[(layer, j)][:, P * a : P * (a + 1)].bitcast(FP8X4),
-                    lhsT_scale=z_scales[(layer, j)][:, P * a : P * (a + 1)],
+                    lhsT=z_codes[r][:, layer, P * a : P * (a + 1)].bitcast(FP8X4),
+                    lhsT_scale=z_scales[r][:, layer, P * a : P * (a + 1)],
                     rhs=w_codes[layer][:, g, :].bitcast(FP8X4),
                     rhs_scale=w_scales[layer][:, g, :],
                     start=(g == 0),
@@ -276,26 +284,45 @@ def tile_cin_pa_kernel(tc, x, x1, w1, b1, w2, b2, out):
                 )
 
         def finish_o1(t):
-            o12[t] = stage.tile([P, LAYERS * S], F32, name="o12", bufs=4)
+            o1[t] = keep.tile([P, S], F32, name="o1_%d" % t)
             nc.vector.tensor_tensor(
-                out=o12[t][:, 0:S].rearrange("p (u r e) -> p u r e", u=2, e=2),
+                out=o1[t][:].rearrange("p (u r e) -> p u r e", u=2, e=2),
                 in0=acc[(0, t)][:].rearrange("p (r u e) -> p u r e", u=2, e=2),
                 in1=b1_rows[:].rearrange("p (u r e) -> p u r e", u=2, e=2),
                 op=ADD,
             )
 
         def finish_o2(t):
-            nc.scalar.copy(out=o12[t][:, S : 2 * S], in_=acc[(1, t)][:])
+            o2[t] = keep.tile([P, S], F32, name="o2_%d" % t)
+            nc.scalar.copy(out=o2[t][:], in_=acc[(1, t)][:])
 
-        def pool_rows(t):
-            window = pool_first - B_TILE * t
-            nc.tensor.matmul(
-                out=pooled[:],
-                lhsT=pool_sel[:, window : window + P],
-                rhs=o12[t][:],
-                start=(t == 0),
-                stop=(t == N_TILES - 1),
+        pooled = {}
+
+        def pool_rows(layer, tiles):
+            if layer not in pooled:
+                pooled[layer] = total.tile([P, S], F32, name="pooled")
+            for t in tiles:
+                window = pool_first - B_TILE * t
+                nc.tensor.matmul(
+                    out=pooled[layer][:],
+                    lhsT=pool_sel[:, window : window + P],
+                    rhs=(o1, o2)[layer][t][:],
+                    start=(t == 0),
+                    stop=(t == N_TILES - 1),
+                )
+
+        def store_o1():
+            result = keep.tile([P, S], F32, name="result1")
+            nc.vector.tensor_copy(
+                out=result[:].rearrange("p (r u e) -> p u r e", u=2, e=2),
+                in_=pooled[0][:].rearrange("p (u r e) -> p u r e", u=2, e=2),
             )
+            nc.sync.dma_start(out=out[:, 0:S], in_=result[0:B, :])
+
+        def store_o2():
+            result = keep.tile([P, S], F32, name="result2")
+            nc.vector.tensor_tensor(out=result[:], in0=pooled[1][:], in1=late_bias[:], op=ADD)
+            nc.sync.dma_start(out=out[:, S : 2 * S], in_=result[0:B, :])
 
         on_scalar = [nc.scalar.copy] * 2
         n_chunks = N_TILES * CHUNKS
@@ -310,7 +337,7 @@ def tile_cin_pa_kernel(tc, x, x1, w1, b1, w2, b2, out):
         for r in range(n_chunks + LEAD + 4):
             k = r - LEAD
             if 0 <= r - 2 < n_chunks:
-                multiply(0, r - 2)
+                multiply(0, r - 2, r - 2)
             if 0 <= k < n_chunks:
                 form_z2(k, SCALAR_BESIDE if r < n_chunks else SCALAR_ALONE)
             if 0 <= k - 4 < n_chunks and (k - 4) % CHUNKS == CHUNKS - 1:
@@ -332,15 +359,22 @@ def tile_cin_pa_kernel(tc, x, x1, w1, b1, w2, b2, out):
             if 0 <= r - 2 < n_chunks and (r - 2) % CHUNKS == CHUNKS - 1:
                 finish_o1((r - 2) // CHUNKS)
             if 0 <= k - 1 < n_chunks:
-                turn_z2(k - 1)
-            if 0 <= r - 1 < n_chunks:
-                quantise(0, r - 1)
-            if 0 <= k - 2 < n_chunks:
-                quantise(1, k - 2)
+                turn_z2(k - 1, r)
+            if 0 <= r - 1 and k - 2 < n_chunks:
+                quantise(r - 1)
             if 0 <= k - 3 < n_chunks:
-                multiply(1, k - 3)
-            if 0 <= k - 4 < n_chunks and (k - 4) % CHUNKS == CHUNKS - 1:
-                pool_rows((k - 4) // CHUNKS)
+                multiply(1, k - 3, r - 2)
+            if r - n_chunks in (3, 4):
+                pool_rows(0, range(4 * (r - n_chunks - 3), 4 * (r - n_chunks - 2)))
+            if r == n_chunks + 5:
+                store_o1()
+            if r == n_chunks + 6:
+                pool_rows(1, range(0, 4))
+            if r == n_chunks + 7:
+                pool_rows(1, range(4, N_TILES - 1))
+            if r == n_chunks + LEAD + 3:
+                pool_rows(1, [N_TILES - 1])
+                store_o2()
             if r in (1, 2, 6, 10, 14, 18):
                 t = (1, 2, 6, 10, 14, 18).index(r) + FIRST_SPREAD
                 if t == FIRST_SPREAD:
@@ -354,11 +388,3 @@ def tile_cin_pa_kernel(tc, x, x1, w1, b1, w2, b2, out):
                 load_x1((3, 10, 18).index(r) + 1)
             if r in (7, 14, 22):
                 group_x1((7, 14, 22).index(r) + 1, nc.scalar.copy)
-
-        result = keep.tile([P, LAYERS * S], F32)
-        nc.vector.tensor_copy(
-            out=result[:, 0:S].rearrange("p (r u e) -> p u r e", u=2, e=2),
-            in_=pooled[:, 0:S].rearrange("p (u r e) -> p u r e", u=2, e=2),
-        )
-        nc.vector.tensor_tensor(out=result[:, S : 2 * S], in0=pooled[:, S : 2 * S], in1=late_bias[:], op=ADD)
-        nc.sync.dma_start(out=out[:, :], in_=result[0:B, :])

@@ -31,7 +31,7 @@ LEAD = 6
 QUARTERS = 4
 B_QUARTER = B // QUARTERS
 N_QUARTER = N // QUARTERS
-SCALAR_BESIDE = 10
+SCALAR_BESIDE = 9
 SCALAR_ALONE = 4
 FIRST_SPREAD = 2
 PINNED = {mybir.EngineType.PE, mybir.EngineType.Activation, mybir.EngineType.DVE}
@@ -332,7 +332,6 @@ def tile_cin_pa_kernel(tc, x, x1, w1, b1, w2, b2, out):
         double_x(0)
         select_x(0)
         turn_x()
-        group_weights(0, 0, [nc.vector.tensor_copy] * 2)
         group_x1(0, nc.vector.tensor_copy)
         for r in range(n_chunks + LEAD + 4):
             k = r - LEAD
@@ -344,6 +343,8 @@ def tile_cin_pa_kernel(tc, x, x1, w1, b1, w2, b2, out):
                 finish_o2((k - 4) // CHUNKS)
             if r < n_chunks:
                 form_z1(r)
+            if r == 0:
+                group_weights(0, 0, [nc.scalar.copy, nc.vector.tensor_copy])
             if r + 1 < n_selected:
                 select_x(r + 1)
             if 1 <= r + 1 < CHUNKS:

@@ -31,7 +31,7 @@ LEAD = 6
 QUARTERS = 4
 B_QUARTER = B // QUARTERS
 N_QUARTER = N // QUARTERS
-SCALAR_BESIDE = 9
+SCALAR_BESIDE = 11
 SCALAR_ALONE = 4
 FIRST_SPREAD = 2
 PINNED = {mybir.EngineType.PE, mybir.EngineType.Activation, mybir.EngineType.DVE}

@@ -31,7 +31,7 @@ LEAD = 6
 QUARTERS = 4
 B_QUARTER = B // QUARTERS
 N_QUARTER = N // QUARTERS
-SCALAR_BESIDE = 11
+SCALAR_BESIDE = 10
 SCALAR_ALONE = 4
 FIRST_SPREAD = 2
 PINNED = {mybir.EngineType.PE, mybir.EngineType.Activation, mybir.EngineType.DVE}
@@ -240,19 +240,25 @@ def tile_cin_pa_kernel(tc, x, x1, w1, b1, w2, b2, out):
                 else:
                     nc.vector.tensor_scalar(out=z_i, in0=o1_t, scalar1=x_i, scalar2=None, op0=MULT)
 
-        def turn_z2(j, r):
-            grouped = grouped_half(r, 1)
+        z_banks = {}
+
+        def turn_z2(j):
             words = rows_n[j][:].bitcast(F32)
-            grouped_words = grouped.bitcast(F32).rearrange("p (a n u) -> p a n u", a=CHUNK, u=2)
+            z_banks[j] = []
             for half in range(CHUNK // 2):
-                bank = turn.tile([P, 2, 2, P], F32, tag="bank")
+                bank = turn.tile([P, 2, 2, P], F32, tag="bank", name="z_bank")
+                z_banks[j].append(bank)
                 for a in range(2):
                     for u in range(2):
                         first = P * (4 * half + 2 * a + u)
                         nc.tensor.transpose(bank[:, a, u, :], words[:, first : first + P], ident_f[:])
-                nc.scalar.copy(
+
+        def copy_z2(j, r, copies):
+            grouped_words = grouped_half(r, 1).bitcast(F32).rearrange("p (a n u) -> p a n u", a=CHUNK, u=2)
+            for half, copy in enumerate(copies):
+                copy(
                     out=grouped_words[:, 2 * half : 2 * half + 2, :, :],
-                    in_=bank[:].rearrange("p a u n -> p a n u"),
+                    in_=z_banks[j][half][:].rearrange("p a u n -> p a n u"),
                 )
 
         def quantise(r):
@@ -325,6 +331,7 @@ def tile_cin_pa_kernel(tc, x, x1, w1, b1, w2, b2, out):
             nc.sync.dma_start(out=out[:, S : 2 * S], in_=result[0:B, :])
 
         on_scalar = [nc.scalar.copy] * 2
+        halves = [nc.scalar.copy, nc.vector.tensor_copy]
         n_chunks = N_TILES * CHUNKS
         n_selected = FIRST_SPREAD * CHUNKS
         stack.enter_context(tc.manual_schedule(engines=PINNED))
@@ -335,16 +342,20 @@ def tile_cin_pa_kernel(tc, x, x1, w1, b1, w2, b2, out):
         group_x1(0, nc.vector.tensor_copy)
         for r in range(n_chunks + LEAD + 4):
             k = r - LEAD
+            if 0 <= k - 1 < n_chunks:
+                turn_z2(k - 1)
             if 0 <= r - 2 < n_chunks:
                 multiply(0, r - 2, r - 2)
             if 0 <= k < n_chunks:
                 form_z2(k, SCALAR_BESIDE if r < n_chunks else SCALAR_ALONE)
-            if 0 <= k - 4 < n_chunks and (k - 4) % CHUNKS == CHUNKS - 1:
-                finish_o2((k - 4) // CHUNKS)
             if r < n_chunks:
                 form_z1(r)
+            if 0 <= r - 2 < n_chunks and (r - 2) % CHUNKS == CHUNKS - 1:
+                finish_o1((r - 2) // CHUNKS)
+            if 0 <= k - 4 < n_chunks and (k - 4) % CHUNKS == CHUNKS - 1:
+                finish_o2((k - 4) // CHUNKS)
             if r == 0:
-                group_weights(0, 0, [nc.scalar.copy, nc.vector.tensor_copy])
+                group_weights(0, 0, halves)
             if r + 1 < n_selected:
                 select_x(r + 1)
             if 1 <= r + 1 < CHUNKS:
@@ -357,22 +368,20 @@ def tile_cin_pa_kernel(tc, x, x1, w1, b1, w2, b2, out):
                 quantise_weights(1, r - 4)
             if r == 3:
                 prepare_biases()
-            if 0 <= r - 2 < n_chunks and (r - 2) % CHUNKS == CHUNKS - 1:
-                finish_o1((r - 2) // CHUNKS)
-            if 0 <= k - 1 < n_chunks:
-                turn_z2(k - 1, r)
-            if 0 <= r - 1 and k - 2 < n_chunks:
-                quantise(r - 1)
+            if r - n_chunks in (2, 3):
+                pool_rows(0, range(4 * (r - n_chunks - 2), 4 * (r - n_chunks - 1)))
+            if r == n_chunks + 5:
+                pool_rows(1, range(0, 4))
+            if r == n_chunks + 6:
+                pool_rows(1, range(4, N_TILES - 1))
             if 0 <= k - 3 < n_chunks:
                 multiply(1, k - 3, r - 2)
-            if r - n_chunks in (3, 4):
-                pool_rows(0, range(4 * (r - n_chunks - 3), 4 * (r - n_chunks - 2)))
-            if r == n_chunks + 5:
+            if 0 <= r - 1 and k - 2 < n_chunks:
+                quantise(r - 1)
+            if 0 <= k - 1 < n_chunks:
+                copy_z2(k - 1, r, on_scalar if k - 1 < n_chunks - 1 else halves)
+            if r == n_chunks + 4:
                 store_o1()
-            if r == n_chunks + 6:
-                pool_rows(1, range(0, 4))
-            if r == n_chunks + 7:
-                pool_rows(1, range(4, N_TILES - 1))
             if r == n_chunks + LEAD + 3:
                 pool_rows(1, [N_TILES - 1])
                 store_o2()

@@ -48,18 +48,24 @@ def tile_cin_pa_kernel(tc, x, x1, w1, b1, w2, b2, out):
         x_fields = keep.tile([P, N // 2], BF16)
         x_twice = keep.tile([P, N // 2, 2], BF16)
 
-        def load_x(h):
-            samples = x[B // 2 * h : B // 2 * (h + 1)].rearrange("b (a q) d -> q a b d", q=QUADS)
+        def load_x(quarter):
+            h, w = divmod(quarter, 2)
+            samples = x[B_QUARTER * quarter : B_QUARTER * (quarter + 1)].rearrange("b (a q) d -> q a b d", q=QUADS)
             for q in range(QUADS):
                 first = F0 * h + PASSES * q
                 nc.sync.dma_start(
-                    out=x_fields[first : first + PASSES, :].rearrange("a (b d) -> a b d", d=D), in_=samples[q]
+                    out=x_fields[first : first + PASSES, N_QUARTER * w : N_QUARTER * (w + 1)].rearrange(
+                        "a (b d) -> a b d", d=D
+                    ),
+                    in_=samples[q],
                 )
 
-        def double_x(w):
-            cols = slice(N_QUARTER * w, N_QUARTER * (w + 1))
+        def double_x(quarter):
+            h, w = divmod(quarter, 2)
+            rows, cols = slice(F0 * h, F0 * (h + 1)), slice(N_QUARTER * w, N_QUARTER * (w + 1))
             nc.vector.tensor_copy(
-                out=x_twice[:, cols, :], in_=x_fields[:, cols].unsqueeze(2).to_broadcast([P, N_QUARTER, 2])
+                out=x_twice[rows, cols, :],
+                in_=x_fields[rows, cols].unsqueeze(2).to_broadcast([F0, N_QUARTER, 2]),
             )
 
         x_spread = [keep.tile([P, PASSES, P, 2], BF16, name="x_spread%d" % t) for t in range(FIRST_SPREAD, N_TILES)]
@@ -84,16 +90,16 @@ def tile_cin_pa_kernel(tc, x, x1, w1, b1, w2, b2, out):
         x1_rows = keep.tile([P, B, 4, D], BF16)
         x1_spread = keep.tile([P, N, 4], BF16)
 
-        def load_x1(quarter):
-            samples = slice(B_QUARTER * quarter, B_QUARTER * (quarter + 1))
+        def load_x1(first, count):
+            samples = slice(first, first + count)
             for q in range(QUADS):
                 nc.sync.dma_start(
                     out=x1_rows[QUAD * q : QUAD * (q + 1), samples, :, :].rearrange("r b t d -> r b (t d)"),
                     in_=x1[samples].rearrange("b (r t) d -> r b (t d)", t=4),
                 )
 
-        def group_x1(quarter, copy):
-            samples = slice(B_QUARTER * quarter, B_QUARTER * (quarter + 1))
+        def group_x1(first, count, copy):
+            samples = slice(first, first + count)
             copy(
                 out=x1_spread[:].rearrange("p (b d) t -> p b d t", d=D)[:, samples, :, :],
                 in_=x1_rows[:, samples, :, :].rearrange("p b t d -> p b d t"),
@@ -109,19 +115,24 @@ def tile_cin_pa_kernel(tc, x, x1, w1, b1, w2, b2, out):
 
         bias_bf = keep.tile([P, LAYERS, S], BF16)
         load_x(0)
-        load_x(1)
-        load_x1(0)
-        for c in range(CHUNKS):
-            load_weights(0, c)
+        load_x1(0, B_TILE)
+        load_weights(0, 0)
+        load_weights(0, 1)
+        load_x1(B_TILE, B_TILE)
+        load_weights(0, 2)
+        load_weights(0, 3)
+        for quarter in range(1, QUARTERS):
+            load_x(quarter)
         nc.sync.dma_start(out=bias_bf[:, 0, :], in_=b1.partition_broadcast(P))
         nc.sync.dma_start(out=bias_bf[:, 1, :], in_=b2.partition_broadcast(P))
-        load_weights(1, 0)
-        load_weights(1, 1)
+        for c in range(CHUNKS):
+            load_weights(1, c)
 
         ident_bf = keep.tile([P, P], BF16)
         make_identity(nc, ident_bf[:])
         ident_f = keep.tile([P, P], F32)
         make_identity(nc, ident_f[:])
+        nc.gpsimd.memset(x_twice[F0:P, 0:N_QUARTER, :], 0.0)
         pool_first = B - B_TILE
         pool_sel = keep.tile([P, pool_first + P], F32)
         nc.vector.memset(pool_sel[:], 0.0)
@@ -338,8 +349,7 @@ def tile_cin_pa_kernel(tc, x, x1, w1, b1, w2, b2, out):
         make_field_sel()
         double_x(0)
         select_x(0)
-        turn_x()
-        group_x1(0, nc.vector.tensor_copy)
+        group_x1(0, B_TILE, nc.vector.tensor_copy)
         for r in range(n_chunks + LEAD + 4):
             k = r - LEAD
             if 0 <= k - 1 < n_chunks:
@@ -356,6 +366,7 @@ def tile_cin_pa_kernel(tc, x, x1, w1, b1, w2, b2, out):
                 finish_o2((k - 4) // CHUNKS)
             if r == 0:
                 group_weights(0, 0, halves)
+                group_x1(B_TILE, B_TILE, nc.vector.tensor_copy)
             if r + 1 < n_selected:
                 select_x(r + 1)
             if 1 <= r + 1 < CHUNKS:
@@ -366,7 +377,8 @@ def tile_cin_pa_kernel(tc, x, x1, w1, b1, w2, b2, out):
                 quantise_weights(0, r)
             if 0 <= r - 4 < CHUNKS:
                 quantise_weights(1, r - 4)
-            if r == 3:
+            if r == 4:
+                turn_x()
                 prepare_biases()
             if r - n_chunks in (2, 3):
                 pool_rows(0, range(4 * (r - n_chunks - 2), 4 * (r - n_chunks - 1)))
@@ -385,16 +397,13 @@ def tile_cin_pa_kernel(tc, x, x1, w1, b1, w2, b2, out):
             if r == n_chunks + LEAD + 3:
                 pool_rows(1, [N_TILES - 1])
                 store_o2()
-            if r in (1, 2, 6, 10, 14, 18):
-                t = (1, 2, 6, 10, 14, 18).index(r) + FIRST_SPREAD
-                if t == FIRST_SPREAD:
-                    double_x(1)
+            if r in (3, 9, 17):
+                double_x((3, 9, 17).index(r) + 1)
+            if r in (3, 4, 9, 13, 17, 21):
+                t = (3, 4, 9, 13, 17, 21).index(r) + FIRST_SPREAD
                 park_x(t)
                 spread_x(t)
-            if r == 1:
-                load_weights(1, 2)
-                load_weights(1, 3)
             if r in (3, 10, 18):
-                load_x1((3, 10, 18).index(r) + 1)
+                load_x1(B_QUARTER * ((3, 10, 18).index(r) + 1), B_QUARTER)
             if r in (7, 14, 22):
-                group_x1((7, 14, 22).index(r) + 1, nc.scalar.copy)
+                group_x1(B_QUARTER * ((7, 14, 22).index(r) + 1), B_QUARTER, nc.scalar.copy)

from contextlib import ExitStack

import concourse.mybir as mybir
from concourse.masks import make_identity

F32 = mybir.dt.float32
BF16 = mybir.dt.bfloat16
U32 = mybir.dt.uint32
U8 = mybir.dt.uint8
FP8X4 = mybir.dt.float8_e4m3fn_x4
MULT = mybir.AluOpType.mult
ADD = mybir.AluOpType.add
COPY = mybir.ActivationFunctionType.Copy

P = 128
B, F0, FK, S, D = 64, 64, 128, 128, 16
N = B * D
K = F0 * FK
K_PASS = 4 * P
PASSES = K // K_PASS
N_TILES = N // P
B_TILE = P // D
CHUNK = 4
CHUNKS = PASSES // CHUNK
I_PASS = K_PASS // FK
I_CHUNK = CHUNK * I_PASS
LAYERS = 2
QUADS = 4
QUAD = P // QUADS
LEAD = 6
QUARTERS = 4
B_QUARTER = B // QUARTERS
N_QUARTER = N // QUARTERS
SCALAR_BESIDE = 10
SCALAR_ALONE = 4
FIRST_SPREAD = 2
PINNED = {mybir.EngineType.PE, mybir.EngineType.Activation, mybir.EngineType.DVE}

FLOPS = LAYERS * 2 * N * K * S


def tile_cin_pa_kernel(tc, x, x1, w1, b1, w2, b2, out):
    nc = tc.nc
    with ExitStack() as stack:
        keep = stack.enter_context(tc.tile_pool(name="keep", bufs=1))
        stage = stack.enter_context(tc.tile_pool(name="stage", bufs=3))

        x_fields = keep.tile([P, N // 2], BF16)
        x_twice = keep.tile([P, N // 2, 2], BF16)

        def load_x(quarter):
            h, w = divmod(quarter, 2)
            samples = x[B_QUARTER * quarter : B_QUARTER * (quarter + 1)].rearrange("b (a q) d -> q a b d", q=QUADS)
            for q in range(QUADS):
                first = F0 * h + PASSES * q
                nc.sync.dma_start(
                    out=x_fields[first : first + PASSES, N_QUARTER * w : N_QUARTER * (w + 1)].rearrange(
                        "a (b d) -> a b d", d=D
                    ),
                    in_=samples[q],
                )

        def double_x(quarter):
            h, w = divmod(quarter, 2)
            rows, cols = slice(F0 * h, F0 * (h + 1)), slice(N_QUARTER * w, N_QUARTER * (w + 1))
            nc.vector.tensor_copy(
                out=x_twice[rows, cols, :],
                in_=x_fields[rows, cols].unsqueeze(2).to_broadcast([F0, N_QUARTER, 2]),
            )

        x_spread = [keep.tile([P, PASSES, P, 2], BF16, name="x_spread%d" % t) for t in range(FIRST_SPREAD, N_TILES)]

        def park_x(t):
            h, m = divmod(t, 4)
            half = out[B // 2 * (t % 2) : B // 2 * (t % 2 + 1), :]
            nc.sync.dma_start(
                out=half.rearrange("r (u n) -> (r u) n", n=P),
                in_=x_twice[F0 * h : F0 * (h + 1), P * m : P * (m + 1), :].rearrange("i n l -> i (n l)").bitcast(F32),
            )

        def spread_x(t):
            half = out[B // 2 * (t % 2) : B // 2 * (t % 2 + 1), :]
            parked = half.rearrange("(q r) n -> q (r n)", q=QUADS)
            words = x_spread[t - FIRST_SPREAD][:].rearrange("p a n l -> p (a n l)").bitcast(F32)
            for q in range(QUADS):
                nc.sync.dma_start(
                    out=words[QUAD * q : QUAD * (q + 1), :], in_=parked[q].partition_broadcast(QUAD)
                )

        x1_rows = keep.tile([P, B, 4, D], BF16)
        x1_spread = keep.tile([P, N, 4], BF16)

        def load_x1(first, count):
            samples = slice(first, first + count)
            for q in range(QUADS):
                nc.sync.dma_start(
                    out=x1_rows[QUAD * q : QUAD * (q + 1), samples, :, :].rearrange("r b t d -> r b (t d)"),
                    in_=x1[samples].rearrange("b (r t) d -> r b (t d)", t=4),
                )

        def group_x1(first, count, copy):
            samples = slice(first, first + count)
            copy(
                out=x1_spread[:].rearrange("p (b d) t -> p b d t", d=D)[:, samples, :, :],
                in_=x1_rows[:, samples, :, :].rearrange("p b t d -> p b d t"),
            )

        w_rows = [keep.tile([P, PASSES, 4, S], BF16, name="w_rows%d" % l) for l in range(LAYERS)]

        def load_weights(layer, c):
            nc.sync.dma_start(
                out=w_rows[layer][:, CHUNK * c : CHUNK * (c + 1), :, :].rearrange("p g t s -> p g (t s)"),
                in_=(w1, w2)[layer].rearrange("(c g p t) s -> p c g (t s)", c=CHUNKS, p=P, t=4)[:, c, :, :],
            )

        bias_bf = keep.tile([P, LAYERS, S], BF16)
        load_x(0)
        load_x1(0, B_TILE)
        load_weights(0, 0)
        load_weights(0, 1)
        load_x1(B_TILE, B_TILE)
        load_weights(0, 2)
        load_weights(0, 3)
        for quarter in range(1, QUARTERS):
            load_x(quarter)
        nc.sync.dma_start(out=bias_bf[:, 0, :], in_=b1.partition_broadcast(P))
        nc.sync.dma_start(out=bias_bf[:, 1, :], in_=b2.partition_broadcast(P))
        for c in range(CHUNKS):
            load_weights(1, c)

        ident_bf = keep.tile([P, P], BF16)
        make_identity(nc, ident_bf[:])
        ident_f = keep.tile([P, P], F32)
        make_identity(nc, ident_f[:])
        nc.gpsimd.memset(x_twice[F0:P, 0:N_QUARTER, :], 0.0)
        pool_first = B - B_TILE
        pool_sel = keep.tile([P, pool_first + P], F32)
        nc.vector.memset(pool_sel[:], 0.0)
        nc.vector.tensor_reduce(
            out=pool_sel[:, pool_first : pool_first + B_TILE],
            in_=ident_f[:].rearrange("p (b d) -> p b d", d=D),
            axis=mybir.AxisListType.X,
            op=ADD,
        )
        turn = stack.enter_context(tc.psum_pool(name="turn", bufs=4))
        sums = stack.enter_context(tc.psum_pool(name="sums", bufs=3))
        total = stack.enter_context(tc.psum_pool(name="total", bufs=1))

        x_scalar = keep.tile([P, 4, 2, QUADS, PASSES], F32)

        def turn_x():
            x_t = turn.tile([P, 4, P], BF16, tag="bank")
            for m in range(4):
                nc.tensor.transpose(x_t[:, m, :], x_fields[:, P * m : P * (m + 1)], ident_bf[:])
            nc.scalar.copy(
                out=x_scalar[:].rearrange("p m h q a -> p (m h q a)"), in_=x_t[:].rearrange("p m c -> p (m c)")
            )

        field_sel = keep.tile([P, PASSES, QUADS, QUAD], BF16)

        def make_field_sel():
            nc.vector.tensor_copy(
                out=field_sel[:],
                in_=ident_bf[:, 0:F0].rearrange("p (q a) -> p a q", q=QUADS).unsqueeze(3)
                .to_broadcast([P, PASSES, QUADS, QUAD]),
            )

        b1_rows = keep.tile([P, S], F32)
        late_bias = keep.tile([P, S], F32)

        def prepare_biases():
            nc.vector.tensor_copy(
                out=b1_rows[:].rearrange("p (u r e) -> p u r e", u=2, e=2),
                in_=bias_bf[:, 0, :].rearrange("p (r u e) -> p u r e", u=2, e=2),
            )
            nc.vector.tensor_scalar(
                out=late_bias[:], in0=bias_bf[:, 1, :], scalar1=float(D), scalar2=None, op0=MULT
            )

        w_codes = [keep.tile([P, PASSES, S], U32, name="w_codes%d" % l, align_bytes=64) for l in range(LAYERS)]
        w_scales = [keep.tile([P, PASSES, S], U8, name="w_scales%d" % l, align_bytes=64) for l in range(LAYERS)]

        w_grouped = {}

        def group_weights(layer, c, copies):
            w_grouped[(layer, c)] = stage.tile([P, CHUNK, S, 4], BF16, align_bytes=64, name="w_grouped", bufs=4)
            for half, copy in enumerate(copies):
                copy(
                    out=w_grouped[(layer, c)][:, 2 * half : 2 * half + 2, :, :],
                    in_=w_rows[layer][:, CHUNK * c + 2 * half : CHUNK * c + 2 * half + 2, :, :]
                    .rearrange("p g t s -> p g s t"),
                )

        def quantise_weights(layer, c):
            chunk = slice(CHUNK * c, CHUNK * (c + 1))
            nc.vector.quantize_mx(
                out=w_codes[layer][:, chunk, :].rearrange("p g s -> p (g s)").bitcast(FP8X4),
                scales=w_scales[layer][:, chunk, :].rearrange("p g s -> p (g s)"),
                in_=w_grouped[(layer, c)][:].rearrange("p g s t -> p (g s t)"),
            )

        rows_n, z_grouped, z_codes, z_scales, acc, o1, o2 = {}, {}, {}, {}, {}, {}, {}

        def grouped_half(r, layer):
            if r not in z_grouped:
                z_grouped[r] = stage.tile([P, LAYERS, CHUNK * P * 4], BF16, name="z_grouped", align_bytes=64)
            return z_grouped[r][:, layer, :]


        x_banks = {}

        def select_x(j):
            t, c = divmod(j, CHUNKS)
            x_banks[j] = turn.tile([P, CHUNK, 2 * P], BF16, tag="bank", name="x_bank")
            for a in range(CHUNK):
                nc.tensor.matmul(
                    out=x_banks[j][:, a, :],
                    lhsT=field_sel[:, CHUNK * c + a, :, :].rearrange("p q r -> p (q r)"),
                    rhs=x_twice[:, P * t : P * (t + 1), :].rearrange("p n l -> p (n l)"),
                    start=True,
                    stop=True,
                )

        def form_z1(j):
            t, c = divmod(j, CHUNKS)
            grouped = grouped_half(j, 0)
            shape = [P, CHUNK * P, 2, 2]
            if t < FIRST_SPREAD:
                x_words = x_banks[j][:].rearrange("p a (n l) -> p (a n) l", l=2)
            else:
                x_words = x_spread[t - FIRST_SPREAD][:, CHUNK * c : CHUNK * (c + 1), :, :].rearrange("p a n l -> p (a n) l")
            nc.vector.tensor_tensor(
                out=grouped.rearrange("p (a w) -> p a w", a=CHUNK),
                in0=x1_spread[:, P * t : P * (t + 1), :].rearrange("p n t -> p (n t)")
                .unsqueeze(1).to_broadcast([P, CHUNK, 4 * P]),
                in1=x_words.unsqueeze(2).to_broadcast(shape),
                op=MULT,
            )

        def form_z2(j, on_scalar):
            t, c = divmod(j, CHUNKS)
            z = stage.tile([P, I_CHUNK * FK], BF16, name="z_rows")
            rows_n[j] = z
            for i in range(I_CHUNK):
                a, q = divmod(i, I_PASS)
                x_i = x_scalar[:, t % 4, t // 4, q, CHUNK * c + a : CHUNK * c + a + 1]
                z_i = z[:, K_PASS * a : K_PASS * (a + 1)].rearrange("p (u q w) -> p u q w", u=2, q=I_PASS)[:, :, q, :]
                o1_t = o1[t][:].rearrange("p (u w) -> p u w", u=2)
                if i * on_scalar % I_CHUNK < on_scalar:
                    nc.scalar.activation(out=z_i, in_=o1_t, func=COPY, scale=x_i)
                else:
                    nc.vector.tensor_scalar(out=z_i, in0=o1_t, scalar1=x_i, scalar2=None, op0=MULT)

        z_banks = {}

        def turn_z2(j):
            words = rows_n[j][:].bitcast(F32)
            z_banks[j] = []
            for half in range(CHUNK // 2):
                bank = turn.tile([P, 2, 2, P], F32, tag="bank", name="z_bank")
                z_banks[j].append(bank)
                for a in range(2):
                    for u in range(2):
                        first = P * (4 * half + 2 * a + u)
                        nc.tensor.transpose(bank[:, a, u, :], words[:, first : first + P], ident_f[:])

        def copy_z2(j, r, copies):
            grouped_words = grouped_half(r, 1).bitcast(F32).rearrange("p (a n u) -> p a n u", a=CHUNK, u=2)
            for half, copy in enumerate(copies):
                copy(
                    out=grouped_words[:, 2 * half : 2 * half + 2, :, :],
                    in_=z_banks[j][half][:].rearrange("p a u n -> p a n u"),
                )

        def quantise(r):
            first = 0 if r < n_chunks else 1
            last = 1 if r - LEAD - 1 >= 0 else 0
            codes = stage.tile([P, LAYERS, CHUNK * P], U32, name="z_codes", align_bytes=64)
            scales = stage.tile([P, LAYERS, CHUNK * P], U8, name="z_scales", align_bytes=64)
            z_codes[r], z_scales[r] = codes, scales
            nc.vector.quantize_mx(
                out=codes[:, first : last + 1, :].rearrange("p l w -> p (l w)").bitcast(FP8X4),
                scales=scales[:, first : last + 1, :].rearrange("p l w -> p (l w)"),
                in_=z_grouped[r][:, first : last + 1, :].rearrange("p l w -> p (l w)"),
            )

        def multiply(layer, j, r):
            t, c = divmod(j, CHUNKS)
            if c == 0:
                acc[(layer, t)] = sums.tile([P, S], F32, name="acc")
            for a in range(CHUNK):
                g = CHUNK * c + a
                nc.tensor.matmul_mx(
                    out=acc[(layer, t)][:],
                    lhsT=z_codes[r][:, layer, P * a : P * (a + 1)].bitcast(FP8X4),
                    lhsT_scale=z_scales[r][:, layer, P * a : P * (a + 1)],
                    rhs=w_codes[layer][:, g, :].bitcast(FP8X4),
                    rhs_scale=w_scales[layer][:, g, :],
                    start=(g == 0),
                    stop=(g == PASSES - 1),
                )

        def finish_o1(t):
            o1[t] = keep.tile([P, S], F32, name="o1_%d" % t)
            nc.vector.tensor_tensor(
                out=o1[t][:].rearrange("p (u r e) -> p u r e", u=2, e=2),
                in0=acc[(0, t)][:].rearrange("p (r u e) -> p u r e", u=2, e=2),
                in1=b1_rows[:].rearrange("p (u r e) -> p u r e", u=2, e=2),
                op=ADD,
            )

        def finish_o2(t):
            o2[t] = keep.tile([P, S], F32, name="o2_%d" % t)
            nc.scalar.copy(out=o2[t][:], in_=acc[(1, t)][:])

        pooled = {}

        def pool_rows(layer, tiles):
            if layer not in pooled:
                pooled[layer] = total.tile([P, S], F32, name="pooled")
            for t in tiles:
                window = pool_first - B_TILE * t
                nc.tensor.matmul(
                    out=pooled[layer][:],
                    lhsT=pool_sel[:, window : window + P],
                    rhs=(o1, o2)[layer][t][:],
                    start=(t == 0),
                    stop=(t == N_TILES - 1),
                )

        def store_o1():
            result = keep.tile([P, S], F32, name="result1")
            nc.vector.tensor_copy(
                out=result[:].rearrange("p (r u e) -> p u r e", u=2, e=2),
                in_=pooled[0][:].rearrange("p (u r e) -> p u r e", u=2, e=2),
            )
            nc.sync.dma_start(out=out[:, 0:S], in_=result[0:B, :])

        def store_o2():
            result = keep.tile([P, S], F32, name="result2")
            nc.vector.tensor_tensor(out=result[:], in0=pooled[1][:], in1=late_bias[:], op=ADD)
            nc.sync.dma_start(out=out[:, S : 2 * S], in_=result[0:B, :])

        on_scalar = [nc.scalar.copy] * 2
        halves = [nc.scalar.copy, nc.vector.tensor_copy]
        n_chunks = N_TILES * CHUNKS
        n_selected = FIRST_SPREAD * CHUNKS
        stack.enter_context(tc.manual_schedule(engines=PINNED))
        make_field_sel()
        double_x(0)
        select_x(0)
        group_x1(0, B_TILE, nc.vector.tensor_copy)
        for r in range(n_chunks + LEAD + 4):
            k = r - LEAD
            if 0 <= k - 1 < n_chunks:
                turn_z2(k - 1)
            if 0 <= r - 2 < n_chunks:
                multiply(0, r - 2, r - 2)
            if 0 <= k < n_chunks:
                form_z2(k, SCALAR_BESIDE if r < n_chunks else SCALAR_ALONE)
            if r < n_chunks:
                form_z1(r)
            if 0 <= r - 2 < n_chunks and (r - 2) % CHUNKS == CHUNKS - 1:
                finish_o1((r - 2) // CHUNKS)
            if 0 <= k - 4 < n_chunks and (k - 4) % CHUNKS == CHUNKS - 1:
                finish_o2((k - 4) // CHUNKS)
            if r == 0:
                group_weights(0, 0, halves)
                group_x1(B_TILE, B_TILE, nc.vector.tensor_copy)
            if r + 1 < n_selected:
                select_x(r + 1)
            if 1 <= r + 1 < CHUNKS:
                group_weights(0, r + 1, on_scalar)
            if 0 <= r - 3 < CHUNKS:
                group_weights(1, r - 3, on_scalar)
            if r < CHUNKS:
                quantise_weights(0, r)
            if 0 <= r - 4 < CHUNKS:
                quantise_weights(1, r - 4)
            if r == 4:
                turn_x()
                prepare_biases()
            if r - n_chunks in (2, 3):
                pool_rows(0, range(4 * (r - n_chunks - 2), 4 * (r - n_chunks - 1)))
            if r == n_chunks + 5:
                pool_rows(1, range(0, 4))
            if r == n_chunks + 6:
                pool_rows(1, range(4, N_TILES - 1))
            if 0 <= k - 3 < n_chunks:
                multiply(1, k - 3, r - 2)
            if 0 <= r - 1 and k - 2 < n_chunks:
                quantise(r - 1)
            if 0 <= k - 1 < n_chunks:
                copy_z2(k - 1, r, on_scalar if k - 1 < n_chunks - 1 else halves)
            if r == n_chunks + 4:
                store_o1()
            if r == n_chunks + LEAD + 3:
                pool_rows(1, [N_TILES - 1])
                store_o2()
            if r in (3, 9, 17):
                double_x((3, 9, 17).index(r) + 1)
            if r in (3, 4, 9, 13, 17, 21):
                t = (3, 4, 9, 13, 17, 21).index(r) + FIRST_SPREAD
                park_x(t)
                spread_x(t)
            if r in (3, 10, 18):
                load_x1(B_QUARTER * ((3, 10, 18).index(r) + 1), B_QUARTER)
            if r in (7, 14, 22):
                group_x1(B_QUARTER * ((7, 14, 22).index(r) + 1), B_QUARTER, nc.scalar.copy)
